import numpy as np
import ml_dtypes


def mxq(x, axis, fmt="e4m3"):
    dtype, down = {"e4m3": (ml_dtypes.float8_e4m3fn, 7), "e5m2": (ml_dtypes.float8_e5m2, 14)}[fmt]
    v = np.moveaxis(np.asarray(x, np.float32).astype(ml_dtypes.bfloat16).astype(np.float64), axis, -1)
    blocks = v.reshape(v.shape[:-1] + (-1, 32))
    amax = np.abs(blocks).max(-1, keepdims=True)
    byte = np.maximum(np.where(amax > 0, np.frexp(amax)[1] - 1 + 127, 0) - down, 1)
    scale = np.exp2(byte - 127.0)
    codes = (blocks / scale).astype(np.float32).astype(dtype).astype(np.float64)
    return np.moveaxis((codes * scale).reshape(v.shape), -1, axis)


WIDE = False


def mx_kscale(k):
    if not WIDE:
        return np.ones(k)
    levels = np.array([10, -10, 5, -5, 0])
    a = np.random.permutation(np.resize(levels, k // 512 * 4)).reshape(k // 512, 4)
    idx = np.arange(k)
    return np.exp2(a[idx // 512, idx % 128 // 32])


BF16 = ml_dtypes.bfloat16


def bf(x):
    return np.asarray(x, np.float32).astype(BF16)


def f64(x):
    return np.asarray(x).astype(np.float64)


E2M1 = np.array([0.0, 0.5, 1.0, 1.5, 2.0, 3.0, 4.0, 6.0, -0.0, -0.5, -1.0, -1.5, -2.0, -3.0, -4.0, -6.0])


def pack_weight(w, fmt):
    k, n = w.shape
    w = f64(bf(w)).reshape(k // 32, 32, n)
    amax = np.abs(w).max(1)
    if fmt == "e4m3":
        byte = np.frexp(amax)[1] - 1 + 127 - 7
    else:
        mant, ex = np.frexp(amax / 6.0)
        byte = np.where(mant > 0.5, ex, ex - 1) + 127
    byte = np.clip(np.where(amax > 0, byte, 1), 1, 254)
    scaled = (w * np.exp2(127.0 - byte)[:, None, :]).reshape(k, n).astype(np.float32)
    by_word = np.ascontiguousarray(scaled.reshape(k // 512, 128, 4, n).transpose(0, 1, 3, 2))
    if fmt == "e4m3":
        words = by_word.astype(ml_dtypes.float8_e4m3fn).view(np.uint8)
    else:
        c = by_word.astype(ml_dtypes.float4_e2m1fn).view(np.uint8) & 0xF
        words = c[..., 0::2] | (c[..., 1::2] << 4)
    return np.ascontiguousarray(words), np.ascontiguousarray(byte.astype(np.uint8).reshape(k // 512, 16, n))


def unpack_weight(words, scales, fmt):
    g, p, n, _ = words.shape
    if fmt == "e4m3":
        vals = np.ascontiguousarray(words).view(ml_dtypes.float8_e4m3fn).astype(np.float64)
    else:
        nib = np.empty((g, p, n, 4), np.uint8)
        nib[..., 0::2] = words & 0xF
        nib[..., 1::2] = words >> 4
        vals = E2M1[nib]
    vals = vals * np.repeat(np.exp2(scales.astype(np.float64) - 127.0), 8, axis=1)[..., None]
    return vals.transpose(0, 1, 3, 2).reshape(g * 512, n)


B, S, D, F, R = 4, 1024, 512, 512, 128
SCALING = 2.0
FMT = "e4m3"


def silu(v):
    return v / (1.0 + np.exp(-v))


def setup_inputs():
    s = mx_kscale(D)
    x = bf(np.random.standard_normal((B, S, D)) * s)
    w1 = np.random.standard_normal((F, D)) / np.sqrt(D) / s
    w3 = np.random.standard_normal((F, D)) / np.sqrt(D) / s
    xa1 = bf(np.random.standard_normal((B, S, R)))
    xa3 = bf(np.random.standard_normal((B, S, R)))
    lora_B1 = bf(np.random.standard_normal((F, R)) * 0.25 / np.sqrt(R))
    lora_B3 = bf(np.random.standard_normal((F, R)) * 0.25 / np.sqrt(R))
    lora_A2 = np.random.standard_normal((R, F)) / np.sqrt(F)
    w1_words, w1_scales = pack_weight(np.ascontiguousarray(w1.T), FMT)
    w3_words, w3_scales = pack_weight(np.ascontiguousarray(w3.T), FMT)
    lora_A2_words, lora_A2_scales = pack_weight(np.ascontiguousarray(lora_A2.T), FMT)
    return {
        "x": x,
        "w1_words": w1_words,
        "w1_scales": w1_scales,
        "w3_words": w3_words,
        "w3_scales": w3_scales,
        "xa1": xa1,
        "xa3": xa3,
        "lora_B1": lora_B1,
        "lora_B3": lora_B3,
        "lora_A2_words": lora_A2_words,
        "lora_A2_scales": lora_A2_scales,
    }


def reference(x, w1_words, w1_scales, w3_words, w3_scales, xa1, xa3, lora_B1, lora_B3, lora_A2_words, lora_A2_scales):
    xq = mxq(f64(x), 2, "e4m3")
    h1 = (xq @ unpack_weight(w1_words, w1_scales, FMT)) + (f64(xa1) @ f64(lora_B1).T) * SCALING
    h3 = (xq @ unpack_weight(w3_words, w3_scales, FMT)) + (f64(xa3) @ f64(lora_B3).T) * SCALING
    g = silu(h1) * h3
    ga2 = mxq(g, 2, "e4m3") @ unpack_weight(lora_A2_words, lora_A2_scales, FMT)
    return g, ga2

@@ -1,0 +1,263 @@
+from contextlib import ExitStack
+
+import concourse.mybir as mybir
+from concourse.masks import make_identity
+
+F32 = mybir.dt.float32
+BF16 = mybir.dt.bfloat16
+I32 = mybir.dt.int32
+U32 = mybir.dt.uint32
+U8 = mybir.dt.uint8
+FP8X4 = mybir.dt.float8_e4m3fn_x4
+ACT = mybir.ActivationFunctionType
+ALU = mybir.AluOpType
+
+P = 128
+PACK = 4
+TOKENS = 4 * 1024
+D = 512
+F = 512
+R = 128
+TILES = TOKENS // P
+GROUP = 4
+GROUPS = TILES // GROUP
+LORA_SCALING = 2.0
+
+PREPARE_AHEAD = 3
+QUANTISE_AHEAD = 2
+TRANSPOSE_BEHIND = 2
+PROJECT_BEHIND = 4
+
+FLOPS = 2 * TOKENS * (2 * D * F + 2 * R * F + F * R)
+
+
+def tile_feedforward_pa_t_kernel(
+    tc,
+    x,
+    w1_words,
+    w1_scales,
+    w3_words,
+    w3_scales,
+    xa1,
+    xa3,
+    lora_B1,
+    lora_B3,
+    lora_A2_words,
+    lora_A2_scales,
+    out_0,
+    out_1,
+):
+    nc = tc.nc
+
+    x_v = x.flatten_outer_dims().rearrange("(p i) d -> p i d", i=TILES)
+    xa1_v = xa1.flatten_outer_dims().rearrange("(p i) r -> p i r", i=TILES)
+    xa3_v = xa3.flatten_outer_dims().rearrange("(p i) r -> p i r", i=TILES)
+    g_v = out_0.flatten_outer_dims().rearrange("(p i) f -> p i f", i=TILES)
+    ga2_v = out_1.flatten_outer_dims().rearrange("(p i) r -> p i r", i=TILES)
+
+    with ExitStack() as ctx:
+        consts = ctx.enter_context(tc.tile_pool(name="consts", bufs=1))
+        inputs = ctx.enter_context(tc.tile_pool(name="inputs", bufs=GROUPS))
+        ahead = ctx.enter_context(tc.tile_pool(name="ahead", bufs=6))
+        work = ctx.enter_context(tc.tile_pool(name="work", bufs=3))
+        behind = ctx.enter_context(tc.tile_pool(name="behind", bufs=5))
+        banks = ctx.enter_context(tc.psum_pool(name="banks", bufs=1))
+        ctx.enter_context(tc.manual_schedule())
+
+        ident_f32 = consts.tile([P, P], F32)
+        make_identity(nc, ident_f32[:])
+        ident_bf = consts.tile([P, P], BF16)
+        make_identity(nc, ident_bf[:])
+
+        warm_in = consts.tile([P, 1], F32)
+        warm_out = consts.tile([P, 1], F32)
+        nc.vector.memset(warm_in[:], 0.0)
+        nc.scalar.activation(out=warm_out[:], in_=warm_in[:], func=ACT.Silu)
+
+        w1_plane = consts.tile([P, F], U8, align_bytes=64)
+        w3_plane = consts.tile([P, F], U8, align_bytes=64)
+        a2_plane = consts.tile([P, R], U8, align_bytes=64)
+        for plane in (w1_plane, w3_plane, a2_plane):
+            nc.vector.memset(plane[:].bitcast(I32), 0)
+
+        x_in = []
+        xa_in = []
+
+        def load_group(grp):
+            tiles = slice(grp * GROUP, (grp + 1) * GROUP)
+            x_g = inputs.tile([P, GROUP, D], BF16, name="x_g")
+            nc.sync.dma_start(out=x_g[:], in_=x_v[:, tiles, :])
+            xa_g = inputs.tile([P, 2, GROUP, R], BF16, name="xa_g")
+            nc.sync.dma_start(out=xa_g[:, 0], in_=xa1_v[:, tiles, :])
+            nc.sync.dma_start(out=xa_g[:, 1], in_=xa3_v[:, tiles, :])
+            x_in.append(x_g)
+            xa_in.append(xa_g)
+
+        def load_scales(plane, scales):
+            for quad in range(4):
+                nc.sync.dma_start(
+                    out=plane[32 * quad : 32 * quad + 4, :].bitcast(I32),
+                    in_=scales[0, 4 * quad : 4 * quad + 4, :].bitcast(I32),
+                )
+
+        def load_words(words_sb, words):
+            nc.sync.dma_start(
+                out=words_sb[:].bitcast(I32),
+                in_=words[0].rearrange("p n t -> p (n t)").bitcast(I32),
+            )
+
+        w1_sb = consts.tile([P, F * PACK], U8, align_bytes=64)
+        w3_sb = consts.tile([P, F * PACK], U8, align_bytes=64)
+        a2_sb = consts.tile([P, R * PACK], U8, align_bytes=64)
+        b_in = consts.tile([P, 2, F // P, R], BF16)
+
+        load_group(0)
+        load_scales(w1_plane, w1_scales)
+        load_words(w1_sb, w1_words)
+        load_scales(w3_plane, w3_scales)
+        load_words(w3_sb, w3_words)
+        nc.sync.dma_start(out=b_in[:, 0], in_=lora_B1.rearrange("(c p) r -> p c r", p=P))
+        nc.sync.dma_start(out=b_in[:, 1], in_=lora_B3.rearrange("(c p) r -> p c r", p=P))
+        load_group(1)
+        load_scales(a2_plane, lora_A2_scales)
+        load_words(a2_sb, lora_A2_words)
+        for grp in range(2, GROUPS):
+            load_group(grp)
+
+        x_grouped = {}
+        x_codes = {}
+        xaT = {}
+        g_tiles = {}
+        g_codes = {}
+        ga2_groups = {}
+        bT = consts.tile([P, 2, F], BF16)
+
+        def transpose_lora_b():
+            bT_ps = banks.tile([P, 2, F], BF16, tag="gT", name="bT_ps")
+            for which in range(2):
+                for c in range(F // P):
+                    nc.tensor.transpose(bT_ps[:, which, c * P : (c + 1) * P], b_in[:, which, c, :], ident_bf[:])
+            nc.vector.tensor_copy(out=bT[:], in_=bT_ps[:])
+
+        def matmuls(i):
+            words, plane = x_codes[i]
+            xaT_sb = xaT[i]
+            mx = []
+            for which, w_sb, w_plane in ((0, w1_sb, w1_plane), (1, w3_sb, w3_plane)):
+                mx_ps = banks.tile([P, F], F32, tag="mx%d" % which, name="mx_ps")
+                nc.tensor.matmul_mx(
+                    out=mx_ps[:],
+                    lhsT=words[:].bitcast(FP8X4),
+                    lhsT_scale=plane[:],
+                    rhs=w_sb[:].bitcast(FP8X4),
+                    rhs_scale=w_plane[:],
+                    start=True,
+                    stop=True,
+                )
+                mx.append(mx_ps)
+            return mx, xaT_sb
+
+        def lora_matmuls(xaT_sb):
+            lora = []
+            for which in range(2):
+                lora_ps = banks.tile([P, F], F32, tag="lora%d" % which, name="lora_ps")
+                nc.tensor.matmul(out=lora_ps[:], lhsT=xaT_sb[:, which, :], rhs=bT[:, which, :], start=True, stop=True)
+                lora.append(lora_ps)
+            return lora
+
+        def project(i, ga2_ps):
+            words, plane = g_codes[i]
+            nc.tensor.matmul_mx(
+                out=ga2_ps[:, i % GROUP, :],
+                lhsT=words[:].bitcast(FP8X4),
+                lhsT_scale=plane[:],
+                rhs=a2_sb[:].bitcast(FP8X4),
+                rhs_scale=a2_plane[:],
+                start=True,
+                stop=True,
+            )
+
+        def one_round(r):
+            gate = 0 <= r < TILES
+            prep = r + PREPARE_AHEAD
+            quant = r + QUANTISE_AHEAD
+            back = r - TRANSPOSE_BEHIND
+            proj = r - PROJECT_BEHIND
+
+            if gate:
+                mx, xaT_sb = matmuls(r)
+            if 0 <= proj < TILES:
+                if proj % GROUP == 0:
+                    ga2_groups["ps"] = banks.tile([P, GROUP, R], F32, name="ga2_ps")
+                    ga2_groups["sb"] = behind.tile([P, GROUP, R], F32, name="ga2_sb", bufs=2)
+                project(proj, ga2_groups["ps"])
+            if gate:
+                lora = lora_matmuls(xaT_sb)
+            if 0 <= back < TILES:
+                gT_ps = banks.tile([P, PACK, P], F32, tag="gT", name="gT_ps")
+                g_back = g_tiles[back]
+                for t in range(PACK):
+                    nc.tensor.transpose(gT_ps[:, t, :], g_back[:, t:F:PACK], ident_f32[:])
+            if 0 <= prep < TILES:
+                x_words = x_in[prep // GROUP][:, prep % GROUP, :].bitcast(F32)
+                xT_ps = banks.tile([P, 2, P], F32, name="xT_ps")
+                for u in range(2):
+                    nc.tensor.transpose(xT_ps[:, u, :], x_words[:, u : D // 2 : 2], ident_f32[:])
+                xaT_ps = banks.tile([P, 2, P], BF16, name="xaT_ps")
+                for which in range(2):
+                    nc.tensor.transpose(xaT_ps[:, which, :], xa_in[prep // GROUP][:, which, prep % GROUP, :], ident_bf[:])
+
+            if gate:
+                h = []
+                for which in range(2):
+                    mx_sb = work.tile([P, F], F32, tag="mx_sb%d" % which, name="mx_sb")
+                    nc.scalar.copy(out=mx_sb[:], in_=mx[which][:])
+                    h_sb = work.tile([P, F], F32, tag="h%d" % which, name="h_sb")
+                    nc.vector.scalar_tensor_tensor(
+                        out=h_sb[:], in0=lora[which][:], scalar=LORA_SCALING, in1=mx_sb[:], op0=ALU.mult, op1=ALU.add
+                    )
+                    h.append(h_sb)
+            if 0 <= proj < TILES:
+                nc.scalar.copy(out=ga2_groups["sb"][:, proj % GROUP, :], in_=ga2_groups["ps"][:, proj % GROUP, :])
+                if proj % GROUP == GROUP - 1:
+                    nc.sync.dma_start(out=ga2_v[:, proj - GROUP + 1 : proj + 1, :], in_=ga2_groups["sb"][:])
+            if gate:
+                s1 = work.tile([P, F], F32, name="s1")
+                nc.scalar.activation(out=s1[:], in_=h[0][:], func=ACT.Silu)
+                g_sb = behind.tile([P, F], F32, name="g_sb")
+                nc.gpsimd.tensor_tensor(out=g_sb[:], in0=s1[:], in1=h[1][:], op=ALU.mult)
+                nc.sync.dma_start(out=g_v[:, r, :], in_=g_sb[:])
+                g_tiles[r] = g_sb
+            if 0 <= prep < TILES:
+                grouped = ahead.tile([P, P * PACK], BF16, align_bytes=64, name="x_grouped")
+                nc.scalar.copy(
+                    out=grouped[:].bitcast(F32).rearrange("p (r u) -> p r u", u=2),
+                    in_=xT_ps[:].rearrange("p u r -> p r u"),
+                )
+                x_grouped[prep] = grouped
+
+            if 0 <= back < TILES:
+                g_grouped = behind.tile([P, P, PACK], BF16, align_bytes=64, name="g_grouped")
+                nc.vector.tensor_copy(out=g_grouped[:], in_=gT_ps[:].rearrange("p t r -> p r t"))
+            if 0 <= quant < TILES:
+                words = ahead.tile([P, P], U32, align_bytes=64, name="x_words_q")
+                plane = ahead.tile([P, P], U8, align_bytes=64, name="x_plane_q")
+                nc.vector.quantize_mx(out=words[:].bitcast(FP8X4), scales=plane[:], in_=x_grouped[quant][:])
+                x_codes[quant] = (words, plane)
+            if 0 <= prep < TILES:
+                xaT_new = ahead.tile([P, 2, P], BF16, name="xaT_sb")
+                nc.vector.tensor_copy(out=xaT_new[:], in_=xaT_ps[:])
+                xaT[prep] = xaT_new
+            if 0 <= back < TILES:
+                words = behind.tile([P, P], U32, align_bytes=64, name="g_words_q")
+                plane = behind.tile([P, P], U8, align_bytes=64, name="g_plane_q")
+                nc.vector.quantize_mx(
+                    out=words[:].bitcast(FP8X4), scales=plane[:], in_=g_grouped[:].rearrange("p r t -> p (r t)")
+                )
+                g_codes[back] = (words, plane)
+
+        for r in range(-PREPARE_AHEAD, 0):
+            one_round(r)
+        transpose_lora_b()
+        for r in range(0, TILES + PROJECT_BEHIND):
+            one_round(r)

@@ -23,10 +23,12 @@ GROUP = 4
 GROUPS = TILES // GROUP
 LORA_SCALING = 2.0
 
-PREPARE_AHEAD = 3
-QUANTISE_AHEAD = 2
-TRANSPOSE_BEHIND = 2
-PROJECT_BEHIND = 4
+PREPARE_AHEAD = 4
+QUANTISE_AHEAD = 3
+LORA_AHEAD = 1
+GATE_BEHIND = 1
+TRANSPOSE_BEHIND = 4
+PROJECT_BEHIND = 6
 
 FLOPS = 2 * TOKENS * (2 * D * F + 2 * R * F + F * R)
 
@@ -60,7 +62,7 @@ def tile_feedforward_pa_t_kernel(
         inputs = ctx.enter_context(tc.tile_pool(name="inputs", bufs=GROUPS))
         ahead = ctx.enter_context(tc.tile_pool(name="ahead", bufs=6))
         work = ctx.enter_context(tc.tile_pool(name="work", bufs=3))
-        behind = ctx.enter_context(tc.tile_pool(name="behind", bufs=5))
+        behind = ctx.enter_context(tc.tile_pool(name="behind", bufs=7))
         banks = ctx.enter_context(tc.psum_pool(name="banks", bufs=1))
         ctx.enter_context(tc.manual_schedule())
 
@@ -127,78 +129,74 @@ def tile_feedforward_pa_t_kernel(
         x_grouped = {}
         x_codes = {}
         xaT = {}
+        lora_sb = {}
+        h_sb = {}
         g_tiles = {}
         g_codes = {}
         ga2_groups = {}
         bT = consts.tile([P, 2, F], BF16)
+        weights = ((w1_sb, w1_plane), (w3_sb, w3_plane))
+
+        def live(i):
+            return 0 <= i < TILES
 
         def transpose_lora_b():
-            bT_ps = banks.tile([P, 2, F], BF16, tag="gT", name="bT_ps")
+            bT_ps = banks.tile([P, 2, F], BF16, tag="gT_ps", name="bT_ps")
             for which in range(2):
                 for c in range(F // P):
                     nc.tensor.transpose(bT_ps[:, which, c * P : (c + 1) * P], b_in[:, which, c, :], ident_bf[:])
             nc.vector.tensor_copy(out=bT[:], in_=bT_ps[:])
 
-        def matmuls(i):
-            words, plane = x_codes[i]
-            xaT_sb = xaT[i]
-            mx = []
-            for which, w_sb, w_plane in ((0, w1_sb, w1_plane), (1, w3_sb, w3_plane)):
-                mx_ps = banks.tile([P, F], F32, tag="mx%d" % which, name="mx_ps")
-                nc.tensor.matmul_mx(
-                    out=mx_ps[:],
-                    lhsT=words[:].bitcast(FP8X4),
-                    lhsT_scale=plane[:],
-                    rhs=w_sb[:].bitcast(FP8X4),
-                    rhs_scale=w_plane[:],
-                    start=True,
-                    stop=True,
-                )
-                mx.append(mx_ps)
-            return mx, xaT_sb
-
-        def lora_matmuls(xaT_sb):
-            lora = []
-            for which in range(2):
-                lora_ps = banks.tile([P, F], F32, tag="lora%d" % which, name="lora_ps")
-                nc.tensor.matmul(out=lora_ps[:], lhsT=xaT_sb[:, which, :], rhs=bT[:, which, :], start=True, stop=True)
-                lora.append(lora_ps)
-            return lora
-
-        def project(i, ga2_ps):
-            words, plane = g_codes[i]
-            nc.tensor.matmul_mx(
-                out=ga2_ps[:, i % GROUP, :],
-                lhsT=words[:].bitcast(FP8X4),
-                lhsT_scale=plane[:],
-                rhs=a2_sb[:].bitcast(FP8X4),
-                rhs_scale=a2_plane[:],
-                start=True,
-                stop=True,
-            )
-
         def one_round(r):
-            gate = 0 <= r < TILES
             prep = r + PREPARE_AHEAD
             quant = r + QUANTISE_AHEAD
+            ahead_tile = r + LORA_AHEAD
+            gate = r - GATE_BEHIND
             back = r - TRANSPOSE_BEHIND
             proj = r - PROJECT_BEHIND
 
-            if gate:
-                mx, xaT_sb = matmuls(r)
-            if 0 <= proj < TILES:
-                if proj % GROUP == 0:
-                    ga2_groups["ps"] = banks.tile([P, GROUP, R], F32, name="ga2_ps")
-                    ga2_groups["sb"] = behind.tile([P, GROUP, R], F32, name="ga2_sb", bufs=2)
-                project(proj, ga2_groups["ps"])
-            if gate:
-                lora = lora_matmuls(xaT_sb)
-            if 0 <= back < TILES:
-                gT_ps = banks.tile([P, PACK, P], F32, tag="gT", name="gT_ps")
-                g_back = g_tiles[back]
+            mx_ps = {}
+            lora_ps = {}
+            for which in range(2):
+                if live(r):
+                    words, plane = x_codes[r]
+                    w_sb, w_plane = weights[which]
+                    mx_ps[which] = banks.tile([P, F], F32, name="mx_ps%d" % which)
+                    nc.tensor.matmul_mx(
+                        out=mx_ps[which][:],
+                        lhsT=words[:].bitcast(FP8X4),
+                        lhsT_scale=plane[:],
+                        rhs=w_sb[:].bitcast(FP8X4),
+                        rhs_scale=w_plane[:],
+                        start=True,
+                        stop=True,
+                    )
+                if live(ahead_tile):
+                    lora_ps[which] = banks.tile([P, F], F32, name="lora_ps%d" % which)
+                    nc.tensor.matmul(
+                        out=lora_ps[which][:],
+                        lhsT=xaT[ahead_tile][:, which, :],
+                        rhs=bT[:, which, :],
+                        start=True,
+                        stop=True,
+                    )
+            if live(proj):
+                words, plane = g_codes[proj]
+                ga2_ps = banks.tile([P, R], F32, name="ga2_ps")
+                nc.tensor.matmul_mx(
+                    out=ga2_ps[:],
+                    lhsT=words[:].bitcast(FP8X4),
+                    lhsT_scale=plane[:],
+                    rhs=a2_sb[:].bitcast(FP8X4),
+                    rhs_scale=a2_plane[:],
+                    start=True,
+                    stop=True,
+                )
+            if live(back):
+                gT_ps = banks.tile([P, PACK, P], F32, name="gT_ps")
                 for t in range(PACK):
-                    nc.tensor.transpose(gT_ps[:, t, :], g_back[:, t:F:PACK], ident_f32[:])
-            if 0 <= prep < TILES:
+                    nc.tensor.transpose(gT_ps[:, t, :], g_tiles[back][:, t:F:PACK], ident_f32[:])
+            if live(prep):
                 x_words = x_in[prep // GROUP][:, prep % GROUP, :].bitcast(F32)
                 xT_ps = banks.tile([P, 2, P], F32, name="xT_ps")
                 for u in range(2):
@@ -207,28 +205,22 @@ def tile_feedforward_pa_t_kernel(
                 for which in range(2):
                     nc.tensor.transpose(xaT_ps[:, which, :], xa_in[prep // GROUP][:, which, prep % GROUP, :], ident_bf[:])
 
-            if gate:
-                h = []
+            if live(gate):
+                s1 = work.tile([P, F], F32, name="s1")
+                nc.scalar.activation(out=s1[:], in_=h_sb[gate][0][:], func=ACT.Silu)
+            if live(ahead_tile):
+                lora_sb[ahead_tile] = []
                 for which in range(2):
-                    mx_sb = work.tile([P, F], F32, tag="mx_sb%d" % which, name="mx_sb")
-                    nc.scalar.copy(out=mx_sb[:], in_=mx[which][:])
-                    h_sb = work.tile([P, F], F32, tag="h%d" % which, name="h_sb")
-                    nc.vector.scalar_tensor_tensor(
-                        out=h_sb[:], in0=lora[which][:], scalar=LORA_SCALING, in1=mx_sb[:], op0=ALU.mult, op1=ALU.add
-                    )
-                    h.append(h_sb)
-            if 0 <= proj < TILES:
-                nc.scalar.copy(out=ga2_groups["sb"][:, proj % GROUP, :], in_=ga2_groups["ps"][:, proj % GROUP, :])
+                    copy_sb = work.tile([P, F], F32, name="lora_sb%d" % which)
+                    nc.scalar.copy(out=copy_sb[:], in_=lora_ps[which][:])
+                    lora_sb[ahead_tile].append(copy_sb)
+            if live(proj):
+                if proj % GROUP == 0:
+                    ga2_groups["sb"] = behind.tile([P, GROUP, R], F32, name="ga2_sb", bufs=2)
+                nc.scalar.copy(out=ga2_groups["sb"][:, proj % GROUP, :], in_=ga2_ps[:])
                 if proj % GROUP == GROUP - 1:
                     nc.sync.dma_start(out=ga2_v[:, proj - GROUP + 1 : proj + 1, :], in_=ga2_groups["sb"][:])
-            if gate:
-                s1 = work.tile([P, F], F32, name="s1")
-                nc.scalar.activation(out=s1[:], in_=h[0][:], func=ACT.Silu)
-                g_sb = behind.tile([P, F], F32, name="g_sb")
-                nc.gpsimd.tensor_tensor(out=g_sb[:], in0=s1[:], in1=h[1][:], op=ALU.mult)
-                nc.sync.dma_start(out=g_v[:, r, :], in_=g_sb[:])
-                g_tiles[r] = g_sb
-            if 0 <= prep < TILES:
+            if live(prep):
                 grouped = ahead.tile([P, P * PACK], BF16, align_bytes=64, name="x_grouped")
                 nc.scalar.copy(
                     out=grouped[:].bitcast(F32).rearrange("p (r u) -> p r u", u=2),
@@ -236,19 +228,38 @@ def tile_feedforward_pa_t_kernel(
                 )
                 x_grouped[prep] = grouped
 
-            if 0 <= back < TILES:
+            if live(gate):
+                g_sb = behind.tile([P, F], F32, name="g_sb")
+                nc.gpsimd.tensor_tensor(out=g_sb[:], in0=s1[:], in1=h_sb[gate][1][:], op=ALU.mult)
+                nc.sync.dma_start(out=g_v[:, gate, :], in_=g_sb[:])
+                g_tiles[gate] = g_sb
+
+            if live(r):
+                h_sb[r] = []
+                for which in range(2):
+                    h = work.tile([P, F], F32, name="h%d" % which, bufs=4)
+                    nc.vector.scalar_tensor_tensor(
+                        out=h[:],
+                        in0=lora_sb[r][which][:],
+                        scalar=LORA_SCALING,
+                        in1=mx_ps[which][:],
+                        op0=ALU.mult,
+                        op1=ALU.add,
+                    )
+                    h_sb[r].append(h)
+            if live(back):
                 g_grouped = behind.tile([P, P, PACK], BF16, align_bytes=64, name="g_grouped")
                 nc.vector.tensor_copy(out=g_grouped[:], in_=gT_ps[:].rearrange("p t r -> p r t"))
-            if 0 <= quant < TILES:
+            if live(quant):
                 words = ahead.tile([P, P], U32, align_bytes=64, name="x_words_q")
                 plane = ahead.tile([P, P], U8, align_bytes=64, name="x_plane_q")
                 nc.vector.quantize_mx(out=words[:].bitcast(FP8X4), scales=plane[:], in_=x_grouped[quant][:])
                 x_codes[quant] = (words, plane)
-            if 0 <= prep < TILES:
+            if live(prep):
                 xaT_new = ahead.tile([P, 2, P], BF16, name="xaT_sb")
                 nc.vector.tensor_copy(out=xaT_new[:], in_=xaT_ps[:])
                 xaT[prep] = xaT_new
-            if 0 <= back < TILES:
+            if live(back):
                 words = behind.tile([P, P], U32, align_bytes=64, name="g_words_q")
                 plane = behind.tile([P, P], U8, align_bytes=64, name="g_plane_q")
                 nc.vector.quantize_mx(
@@ -256,8 +267,8 @@ def tile_feedforward_pa_t_kernel(
                 )
                 g_codes[back] = (words, plane)
 
-        for r in range(-PREPARE_AHEAD, 0):
+        for r in range(-PREPARE_AHEAD, -LORA_AHEAD):
             one_round(r)
         transpose_lora_b()
-        for r in range(0, TILES + PROJECT_BEHIND):
+        for r in range(-LORA_AHEAD, TILES + PROJECT_BEHIND):
             one_round(r)

@@ -23,12 +23,13 @@ GROUP = 4
 GROUPS = TILES // GROUP
 LORA_SCALING = 2.0
 
-PREPARE_AHEAD = 4
-QUANTISE_AHEAD = 3
+PREPARE_AHEAD = 5
+QUANTISE_AHEAD = 4
 LORA_AHEAD = 1
-GATE_BEHIND = 1
 TRANSPOSE_BEHIND = 4
-PROJECT_BEHIND = 6
+REQUANTISE_BEHIND = 5
+PROJECT_BEHIND = 7
+BANKS = 8
 
 FLOPS = 2 * TOKENS * (2 * D * F + 2 * R * F + F * R)
 
@@ -60,7 +61,7 @@ def tile_feedforward_pa_t_kernel(
     with ExitStack() as ctx:
         consts = ctx.enter_context(tc.tile_pool(name="consts", bufs=1))
         inputs = ctx.enter_context(tc.tile_pool(name="inputs", bufs=GROUPS))
-        ahead = ctx.enter_context(tc.tile_pool(name="ahead", bufs=6))
+        ahead = ctx.enter_context(tc.tile_pool(name="ahead", bufs=7))
         work = ctx.enter_context(tc.tile_pool(name="work", bufs=3))
         behind = ctx.enter_context(tc.tile_pool(name="behind", bufs=7))
         banks = ctx.enter_context(tc.psum_pool(name="banks", bufs=1))
@@ -130,142 +131,135 @@ def tile_feedforward_pa_t_kernel(
         x_codes = {}
         xaT = {}
         lora_sb = {}
-        h_sb = {}
         g_tiles = {}
+        g_grouped = {}
         g_codes = {}
         ga2_groups = {}
         bT = consts.tile([P, 2, F], BF16)
         weights = ((w1_sb, w1_plane), (w3_sb, w3_plane))
+        bank_count = []
 
         def live(i):
             return 0 <= i < TILES
 
+        def next_bank(shape, dtype):
+            bank_count.append(1)
+            return banks.tile(shape, dtype, tag="bank%d" % (len(bank_count) % BANKS), name="ps")
+
         def transpose_lora_b():
-            bT_ps = banks.tile([P, 2, F], BF16, tag="gT_ps", name="bT_ps")
+            bT_ps = next_bank([P, 2, F], BF16)
             for which in range(2):
                 for c in range(F // P):
                     nc.tensor.transpose(bT_ps[:, which, c * P : (c + 1) * P], b_in[:, which, c, :], ident_bf[:])
             nc.vector.tensor_copy(out=bT[:], in_=bT_ps[:])
 
+        def lora_matmul(i, which):
+            lora_ps = next_bank([P, F], F32)
+            nc.tensor.matmul(out=lora_ps[:], lhsT=xaT[i][:, which, :], rhs=bT[:, which, :], start=True, stop=True)
+            return lora_ps
+
+        def mx_matmul(codes, w_sb, w_plane, width):
+            words, plane = codes
+            out_ps = next_bank([P, width], F32)
+            nc.tensor.matmul_mx(
+                out=out_ps[:],
+                lhsT=words[:].bitcast(FP8X4),
+                lhsT_scale=plane[:],
+                rhs=w_sb[:].bitcast(FP8X4),
+                rhs_scale=w_plane[:],
+                start=True,
+                stop=True,
+            )
+            return out_ps
+
+        def quantise(pool, grouped, name):
+            words = pool.tile([P, P], U32, align_bytes=64, name=name + "_words")
+            plane = pool.tile([P, P], U8, align_bytes=64, name=name + "_plane")
+            nc.vector.quantize_mx(out=words[:].bitcast(FP8X4), scales=plane[:], in_=grouped)
+            return words, plane
+
         def one_round(r):
             prep = r + PREPARE_AHEAD
             quant = r + QUANTISE_AHEAD
             ahead_tile = r + LORA_AHEAD
-            gate = r - GATE_BEHIND
             back = r - TRANSPOSE_BEHIND
+            requant = r - REQUANTISE_BEHIND
             proj = r - PROJECT_BEHIND
 
-            mx_ps = {}
             lora_ps = {}
-            for which in range(2):
-                if live(r):
-                    words, plane = x_codes[r]
-                    w_sb, w_plane = weights[which]
-                    mx_ps[which] = banks.tile([P, F], F32, name="mx_ps%d" % which)
-                    nc.tensor.matmul_mx(
-                        out=mx_ps[which][:],
-                        lhsT=words[:].bitcast(FP8X4),
-                        lhsT_scale=plane[:],
-                        rhs=w_sb[:].bitcast(FP8X4),
-                        rhs_scale=w_plane[:],
-                        start=True,
-                        stop=True,
-                    )
-                if live(ahead_tile):
-                    lora_ps[which] = banks.tile([P, F], F32, name="lora_ps%d" % which)
-                    nc.tensor.matmul(
-                        out=lora_ps[which][:],
-                        lhsT=xaT[ahead_tile][:, which, :],
-                        rhs=bT[:, which, :],
-                        start=True,
-                        stop=True,
-                    )
+            mx_ps = {}
+            if live(ahead_tile):
+                lora_ps[0] = lora_matmul(ahead_tile, 0)
             if live(proj):
-                words, plane = g_codes[proj]
-                ga2_ps = banks.tile([P, R], F32, name="ga2_ps")
-                nc.tensor.matmul_mx(
-                    out=ga2_ps[:],
-                    lhsT=words[:].bitcast(FP8X4),
-                    lhsT_scale=plane[:],
-                    rhs=a2_sb[:].bitcast(FP8X4),
-                    rhs_scale=a2_plane[:],
-                    start=True,
-                    stop=True,
-                )
-            if live(back):
-                gT_ps = banks.tile([P, PACK, P], F32, name="gT_ps")
-                for t in range(PACK):
-                    nc.tensor.transpose(gT_ps[:, t, :], g_tiles[back][:, t:F:PACK], ident_f32[:])
+                ga2_ps = mx_matmul(g_codes[proj], a2_sb, a2_plane, R)
+            if live(r):
+                for which in range(2):
+                    mx_ps[which] = mx_matmul(x_codes[r], weights[which][0], weights[which][1], F)
+            if live(ahead_tile):
+                lora_ps[1] = lora_matmul(ahead_tile, 1)
             if live(prep):
+                in_ps = next_bank([P, 3 * P], F32)
+                xT_ps = in_ps[:, 0 : 2 * P].rearrange("p (u r) -> p u r", u=2)
+                xaT_ps = in_ps[:, 2 * P : 3 * P].bitcast(BF16).rearrange("p (w r) -> p w r", w=2)
                 x_words = x_in[prep // GROUP][:, prep % GROUP, :].bitcast(F32)
-                xT_ps = banks.tile([P, 2, P], F32, name="xT_ps")
                 for u in range(2):
                     nc.tensor.transpose(xT_ps[:, u, :], x_words[:, u : D // 2 : 2], ident_f32[:])
-                xaT_ps = banks.tile([P, 2, P], BF16, name="xaT_ps")
                 for which in range(2):
                     nc.tensor.transpose(xaT_ps[:, which, :], xa_in[prep // GROUP][:, which, prep % GROUP, :], ident_bf[:])
+            if live(back):
+                gT_ps = next_bank([P, PACK, P], F32)
+                for t in range(PACK):
+                    nc.tensor.transpose(gT_ps[:, t, :], g_tiles[back][:, t:F:PACK], ident_f32[:])
 
-            if live(gate):
-                s1 = work.tile([P, F], F32, name="s1")
-                nc.scalar.activation(out=s1[:], in_=h_sb[gate][0][:], func=ACT.Silu)
-            if live(ahead_tile):
-                lora_sb[ahead_tile] = []
-                for which in range(2):
-                    copy_sb = work.tile([P, F], F32, name="lora_sb%d" % which)
-                    nc.scalar.copy(out=copy_sb[:], in_=lora_ps[which][:])
-                    lora_sb[ahead_tile].append(copy_sb)
             if live(proj):
                 if proj % GROUP == 0:
                     ga2_groups["sb"] = behind.tile([P, GROUP, R], F32, name="ga2_sb", bufs=2)
                 nc.scalar.copy(out=ga2_groups["sb"][:, proj % GROUP, :], in_=ga2_ps[:])
                 if proj % GROUP == GROUP - 1:
                     nc.sync.dma_start(out=ga2_v[:, proj - GROUP + 1 : proj + 1, :], in_=ga2_groups["sb"][:])
+            if live(ahead_tile):
+                lora_sb[ahead_tile] = []
+                for which in range(2):
+                    copy_sb = work.tile([P, F], F32, name="lora_sb%d" % which)
+                    nc.scalar.copy(out=copy_sb[:], in_=lora_ps[which][:])
+                    lora_sb[ahead_tile].append(copy_sb)
             if live(prep):
                 grouped = ahead.tile([P, P * PACK], BF16, align_bytes=64, name="x_grouped")
                 nc.scalar.copy(
                     out=grouped[:].bitcast(F32).rearrange("p (r u) -> p r u", u=2),
-                    in_=xT_ps[:].rearrange("p u r -> p r u"),
+                    in_=xT_ps.rearrange("p u r -> p r u"),
                 )
                 x_grouped[prep] = grouped
+                xaT[prep] = ahead.tile([P, 2, P], BF16, name="xaT_sb")
+                nc.scalar.copy(out=xaT[prep][:], in_=xaT_ps)
 
-            if live(gate):
-                g_sb = behind.tile([P, F], F32, name="g_sb")
-                nc.gpsimd.tensor_tensor(out=g_sb[:], in0=s1[:], in1=h_sb[gate][1][:], op=ALU.mult)
-                nc.sync.dma_start(out=g_v[:, gate, :], in_=g_sb[:])
-                g_tiles[gate] = g_sb
-
+            if live(requant):
+                g_codes[requant] = quantise(behind, g_grouped[requant][:].rearrange("p r t -> p (r t)"), "g")
             if live(r):
-                h_sb[r] = []
+                h = []
                 for which in range(2):
-                    h = work.tile([P, F], F32, name="h%d" % which, bufs=4)
+                    h_sb = work.tile([P, F], F32, name="h%d" % which)
                     nc.vector.scalar_tensor_tensor(
-                        out=h[:],
+                        out=h_sb[:],
                         in0=lora_sb[r][which][:],
                         scalar=LORA_SCALING,
                         in1=mx_ps[which][:],
                         op0=ALU.mult,
                         op1=ALU.add,
                     )
-                    h_sb[r].append(h)
-            if live(back):
-                g_grouped = behind.tile([P, P, PACK], BF16, align_bytes=64, name="g_grouped")
-                nc.vector.tensor_copy(out=g_grouped[:], in_=gT_ps[:].rearrange("p t r -> p r t"))
+                    h.append(h_sb)
             if live(quant):
-                words = ahead.tile([P, P], U32, align_bytes=64, name="x_words_q")
-                plane = ahead.tile([P, P], U8, align_bytes=64, name="x_plane_q")
-                nc.vector.quantize_mx(out=words[:].bitcast(FP8X4), scales=plane[:], in_=x_grouped[quant][:])
-                x_codes[quant] = (words, plane)
-            if live(prep):
-                xaT_new = ahead.tile([P, 2, P], BF16, name="xaT_sb")
-                nc.vector.tensor_copy(out=xaT_new[:], in_=xaT_ps[:])
-                xaT[prep] = xaT_new
+                x_codes[quant] = quantise(ahead, x_grouped[quant][:], "x")
             if live(back):
-                words = behind.tile([P, P], U32, align_bytes=64, name="g_words_q")
-                plane = behind.tile([P, P], U8, align_bytes=64, name="g_plane_q")
-                nc.vector.quantize_mx(
-                    out=words[:].bitcast(FP8X4), scales=plane[:], in_=g_grouped[:].rearrange("p r t -> p (r t)")
-                )
-                g_codes[back] = (words, plane)
+                g_grouped[back] = behind.tile([P, P, PACK], BF16, align_bytes=64, name="g_grouped")
+                nc.vector.tensor_copy(out=g_grouped[back][:], in_=gT_ps[:].rearrange("p t r -> p r t"))
+
+            if live(r):
+                s1 = work.tile([P, F], F32, name="s1")
+                nc.scalar.activation(out=s1[:], in_=h[0][:], func=ACT.Silu)
+                g_tiles[r] = behind.tile([P, F], F32, name="g_sb")
+                nc.gpsimd.tensor_tensor(out=g_tiles[r][:], in0=s1[:], in1=h[1][:], op=ALU.mult)
+                nc.sync.dma_start(out=g_v[:, r, :], in_=g_tiles[r][:])
 
         for r in range(-PREPARE_AHEAD, -LORA_AHEAD):
             one_round(r)

@@ -23,13 +23,12 @@ GROUP = 4
 GROUPS = TILES // GROUP
 LORA_SCALING = 2.0
 
-PREPARE_AHEAD = 5
-QUANTISE_AHEAD = 4
+PREPARE_AHEAD = 4
+QUANTISE_AHEAD = 3
 LORA_AHEAD = 1
+GATE_BEHIND = 1
 TRANSPOSE_BEHIND = 4
-REQUANTISE_BEHIND = 5
-PROJECT_BEHIND = 7
-BANKS = 8
+PROJECT_BEHIND = 6
 
 FLOPS = 2 * TOKENS * (2 * D * F + 2 * R * F + F * R)
 
@@ -61,7 +60,7 @@ def tile_feedforward_pa_t_kernel(
     with ExitStack() as ctx:
         consts = ctx.enter_context(tc.tile_pool(name="consts", bufs=1))
         inputs = ctx.enter_context(tc.tile_pool(name="inputs", bufs=GROUPS))
-        ahead = ctx.enter_context(tc.tile_pool(name="ahead", bufs=7))
+        ahead = ctx.enter_context(tc.tile_pool(name="ahead", bufs=6))
         work = ctx.enter_context(tc.tile_pool(name="work", bufs=3))
         behind = ctx.enter_context(tc.tile_pool(name="behind", bufs=7))
         banks = ctx.enter_context(tc.psum_pool(name="banks", bufs=1))
@@ -131,135 +130,148 @@ def tile_feedforward_pa_t_kernel(
         x_codes = {}
         xaT = {}
         lora_sb = {}
+        h_sb = {}
         g_tiles = {}
-        g_grouped = {}
         g_codes = {}
         ga2_groups = {}
         bT = consts.tile([P, 2, F], BF16)
         weights = ((w1_sb, w1_plane), (w3_sb, w3_plane))
-        bank_count = []
 
         def live(i):
             return 0 <= i < TILES
 
-        def next_bank(shape, dtype):
-            bank_count.append(1)
-            return banks.tile(shape, dtype, tag="bank%d" % (len(bank_count) % BANKS), name="ps")
-
         def transpose_lora_b():
-            bT_ps = next_bank([P, 2, F], BF16)
+            bT_ps = banks.tile([P, 2, F], BF16, tag="gT_ps", name="bT_ps")
             for which in range(2):
                 for c in range(F // P):
                     nc.tensor.transpose(bT_ps[:, which, c * P : (c + 1) * P], b_in[:, which, c, :], ident_bf[:])
             nc.vector.tensor_copy(out=bT[:], in_=bT_ps[:])
 
-        def lora_matmul(i, which):
-            lora_ps = next_bank([P, F], F32)
-            nc.tensor.matmul(out=lora_ps[:], lhsT=xaT[i][:, which, :], rhs=bT[:, which, :], start=True, stop=True)
-            return lora_ps
-
-        def mx_matmul(codes, w_sb, w_plane, width):
-            words, plane = codes
-            out_ps = next_bank([P, width], F32)
-            nc.tensor.matmul_mx(
-                out=out_ps[:],
-                lhsT=words[:].bitcast(FP8X4),
-                lhsT_scale=plane[:],
-                rhs=w_sb[:].bitcast(FP8X4),
-                rhs_scale=w_plane[:],
-                start=True,
-                stop=True,
-            )
-            return out_ps
-
-        def quantise(pool, grouped, name):
-            words = pool.tile([P, P], U32, align_bytes=64, name=name + "_words")
-            plane = pool.tile([P, P], U8, align_bytes=64, name=name + "_plane")
-            nc.vector.quantize_mx(out=words[:].bitcast(FP8X4), scales=plane[:], in_=grouped)
-            return words, plane
-
         def one_round(r):
             prep = r + PREPARE_AHEAD
             quant = r + QUANTISE_AHEAD
             ahead_tile = r + LORA_AHEAD
+            gate = r - GATE_BEHIND
             back = r - TRANSPOSE_BEHIND
-            requant = r - REQUANTISE_BEHIND
             proj = r - PROJECT_BEHIND
 
-            lora_ps = {}
             mx_ps = {}
+            lora_ps = {}
+
+            def lora_matmul(which):
+                lora_ps[which] = banks.tile([P, F], F32, name="lora_ps%d" % which)
+                nc.tensor.matmul(
+                    out=lora_ps[which][:],
+                    lhsT=xaT[ahead_tile][:, which, :],
+                    rhs=bT[:, which, :],
+                    start=True,
+                    stop=True,
+                )
+
             if live(ahead_tile):
-                lora_ps[0] = lora_matmul(ahead_tile, 0)
+                lora_matmul(0)
+            for which in range(2):
+                if live(r):
+                    words, plane = x_codes[r]
+                    w_sb, w_plane = weights[which]
+                    mx_ps[which] = banks.tile([P, F], F32, name="mx_ps%d" % which)
+                    nc.tensor.matmul_mx(
+                        out=mx_ps[which][:],
+                        lhsT=words[:].bitcast(FP8X4),
+                        lhsT_scale=plane[:],
+                        rhs=w_sb[:].bitcast(FP8X4),
+                        rhs_scale=w_plane[:],
+                        start=True,
+                        stop=True,
+                    )
             if live(proj):
-                ga2_ps = mx_matmul(g_codes[proj], a2_sb, a2_plane, R)
-            if live(r):
-                for which in range(2):
-                    mx_ps[which] = mx_matmul(x_codes[r], weights[which][0], weights[which][1], F)
+                words, plane = g_codes[proj]
+                ga2_ps = banks.tile([P, R], F32, name="ga2_ps")
+                nc.tensor.matmul_mx(
+                    out=ga2_ps[:],
+                    lhsT=words[:].bitcast(FP8X4),
+                    lhsT_scale=plane[:],
+                    rhs=a2_sb[:].bitcast(FP8X4),
+                    rhs_scale=a2_plane[:],
+                    start=True,
+                    stop=True,
+                )
             if live(ahead_tile):
-                lora_ps[1] = lora_matmul(ahead_tile, 1)
-            if live(prep):
-                in_ps = next_bank([P, 3 * P], F32)
-                xT_ps = in_ps[:, 0 : 2 * P].rearrange("p (u r) -> p u r", u=2)
-                xaT_ps = in_ps[:, 2 * P : 3 * P].bitcast(BF16).rearrange("p (w r) -> p w r", w=2)
-                x_words = x_in[prep // GROUP][:, prep % GROUP, :].bitcast(F32)
-                for u in range(2):
-                    nc.tensor.transpose(xT_ps[:, u, :], x_words[:, u : D // 2 : 2], ident_f32[:])
-                for which in range(2):
-                    nc.tensor.transpose(xaT_ps[:, which, :], xa_in[prep // GROUP][:, which, prep % GROUP, :], ident_bf[:])
+                lora_matmul(1)
             if live(back):
-                gT_ps = next_bank([P, PACK, P], F32)
+                gT_ps = banks.tile([P, PACK, P], F32, name="gT_ps")
                 for t in range(PACK):
                     nc.tensor.transpose(gT_ps[:, t, :], g_tiles[back][:, t:F:PACK], ident_f32[:])
+            if live(prep):
+                x_words = x_in[prep // GROUP][:, prep % GROUP, :].bitcast(F32)
+                xT_ps = banks.tile([P, 2, P], F32, name="xT_ps")
+                for u in range(2):
+                    nc.tensor.transpose(xT_ps[:, u, :], x_words[:, u : D // 2 : 2], ident_f32[:])
+                xaT_ps = banks.tile([P, 2, P], BF16, name="xaT_ps")
+                for which in range(2):
+                    nc.tensor.transpose(xaT_ps[:, which, :], xa_in[prep // GROUP][:, which, prep % GROUP, :], ident_bf[:])
 
-            if live(proj):
-                if proj % GROUP == 0:
-                    ga2_groups["sb"] = behind.tile([P, GROUP, R], F32, name="ga2_sb", bufs=2)
-                nc.scalar.copy(out=ga2_groups["sb"][:, proj % GROUP, :], in_=ga2_ps[:])
-                if proj % GROUP == GROUP - 1:
-                    nc.sync.dma_start(out=ga2_v[:, proj - GROUP + 1 : proj + 1, :], in_=ga2_groups["sb"][:])
+            if live(gate):
+                s1 = work.tile([P, F], F32, name="s1")
+                nc.scalar.activation(out=s1[:], in_=h_sb[gate][0][:], func=ACT.Silu)
             if live(ahead_tile):
                 lora_sb[ahead_tile] = []
                 for which in range(2):
                     copy_sb = work.tile([P, F], F32, name="lora_sb%d" % which)
                     nc.scalar.copy(out=copy_sb[:], in_=lora_ps[which][:])
                     lora_sb[ahead_tile].append(copy_sb)
+            if live(proj):
+                if proj % GROUP == 0:
+                    ga2_groups["sb"] = behind.tile([P, GROUP, R], F32, name="ga2_sb", bufs=2)
+                nc.scalar.copy(out=ga2_groups["sb"][:, proj % GROUP, :], in_=ga2_ps[:])
+                if proj % GROUP == GROUP - 1:
+                    nc.sync.dma_start(out=ga2_v[:, proj - GROUP + 1 : proj + 1, :], in_=ga2_groups["sb"][:])
             if live(prep):
                 grouped = ahead.tile([P, P * PACK], BF16, align_bytes=64, name="x_grouped")
                 nc.scalar.copy(
                     out=grouped[:].bitcast(F32).rearrange("p (r u) -> p r u", u=2),
-                    in_=xT_ps.rearrange("p u r -> p r u"),
+                    in_=xT_ps[:].rearrange("p u r -> p r u"),
                 )
                 x_grouped[prep] = grouped
-                xaT[prep] = ahead.tile([P, 2, P], BF16, name="xaT_sb")
-                nc.scalar.copy(out=xaT[prep][:], in_=xaT_ps)
 
-            if live(requant):
-                g_codes[requant] = quantise(behind, g_grouped[requant][:].rearrange("p r t -> p (r t)"), "g")
+            if live(gate):
+                g_sb = behind.tile([P, F], F32, name="g_sb")
+                nc.gpsimd.tensor_tensor(out=g_sb[:], in0=s1[:], in1=h_sb[gate][1][:], op=ALU.mult)
+                nc.sync.dma_start(out=g_v[:, gate, :], in_=g_sb[:])
+                g_tiles[gate] = g_sb
+
             if live(r):
-                h = []
+                h_sb[r] = []
                 for which in range(2):
-                    h_sb = work.tile([P, F], F32, name="h%d" % which)
+                    h = work.tile([P, F], F32, name="h%d" % which, bufs=4)
                     nc.vector.scalar_tensor_tensor(
-                        out=h_sb[:],
+                        out=h[:],
                         in0=lora_sb[r][which][:],
                         scalar=LORA_SCALING,
                         in1=mx_ps[which][:],
                         op0=ALU.mult,
                         op1=ALU.add,
                     )
-                    h.append(h_sb)
-            if live(quant):
-                x_codes[quant] = quantise(ahead, x_grouped[quant][:], "x")
+                    h_sb[r].append(h)
             if live(back):
-                g_grouped[back] = behind.tile([P, P, PACK], BF16, align_bytes=64, name="g_grouped")
-                nc.vector.tensor_copy(out=g_grouped[back][:], in_=gT_ps[:].rearrange("p t r -> p r t"))
-
-            if live(r):
-                s1 = work.tile([P, F], F32, name="s1")
-                nc.scalar.activation(out=s1[:], in_=h[0][:], func=ACT.Silu)
-                g_tiles[r] = behind.tile([P, F], F32, name="g_sb")
-                nc.gpsimd.tensor_tensor(out=g_tiles[r][:], in0=s1[:], in1=h[1][:], op=ALU.mult)
-                nc.sync.dma_start(out=g_v[:, r, :], in_=g_tiles[r][:])
+                g_grouped = behind.tile([P, P, PACK], BF16, align_bytes=64, name="g_grouped")
+                nc.vector.tensor_copy(out=g_grouped[:], in_=gT_ps[:].rearrange("p t r -> p r t"))
+            if live(quant):
+                words = ahead.tile([P, P], U32, align_bytes=64, name="x_words_q")
+                plane = ahead.tile([P, P], U8, align_bytes=64, name="x_plane_q")
+                nc.vector.quantize_mx(out=words[:].bitcast(FP8X4), scales=plane[:], in_=x_grouped[quant][:])
+                x_codes[quant] = (words, plane)
+            if live(prep):
+                xaT_new = ahead.tile([P, 2, P], BF16, name="xaT_sb")
+                nc.vector.tensor_copy(out=xaT_new[:], in_=xaT_ps[:])
+                xaT[prep] = xaT_new
+            if live(back):
+                words = behind.tile([P, P], U32, align_bytes=64, name="g_words_q")
+                plane = behind.tile([P, P], U8, align_bytes=64, name="g_plane_q")
+                nc.vector.quantize_mx(
+                    out=words[:].bitcast(FP8X4), scales=plane[:], in_=g_grouped[:].rearrange("p r t -> p (r t)")
+                )
+                g_codes[back] = (words, plane)
 
         for r in range(-PREPARE_AHEAD, -LORA_AHEAD):
             one_round(r)

@@ -66,10 +66,10 @@ def tile_feedforward_pa_t_kernel(
         banks = ctx.enter_context(tc.psum_pool(name="banks", bufs=1))
         ctx.enter_context(tc.manual_schedule())
 
-        ident_f32 = consts.tile([P, P], F32)
-        make_identity(nc, ident_f32[:])
         ident_bf = consts.tile([P, P], BF16)
         make_identity(nc, ident_bf[:])
+        ident_f32 = consts.tile([P, P], F32)
+        make_identity(nc, ident_f32[:])
 
         warm_in = consts.tile([P, 1], F32)
         warm_out = consts.tile([P, 1], F32)
@@ -113,13 +113,13 @@ def tile_feedforward_pa_t_kernel(
         a2_sb = consts.tile([P, R * PACK], U8, align_bytes=64)
         b_in = consts.tile([P, 2, F // P, R], BF16)
 
-        load_group(0)
-        load_scales(w1_plane, w1_scales)
-        load_words(w1_sb, w1_words)
-        load_scales(w3_plane, w3_scales)
-        load_words(w3_sb, w3_words)
         nc.sync.dma_start(out=b_in[:, 0], in_=lora_B1.rearrange("(c p) r -> p c r", p=P))
         nc.sync.dma_start(out=b_in[:, 1], in_=lora_B3.rearrange("(c p) r -> p c r", p=P))
+        load_group(0)
+        load_words(w1_sb, w1_words)
+        load_words(w3_sb, w3_words)
+        load_scales(w1_plane, w1_scales)
+        load_scales(w3_plane, w3_scales)
         load_group(1)
         load_scales(a2_plane, lora_A2_scales)
         load_words(a2_sb, lora_A2_words)
@@ -273,8 +273,6 @@ def tile_feedforward_pa_t_kernel(
                 )
                 g_codes[back] = (words, plane)
 
-        for r in range(-PREPARE_AHEAD, -LORA_AHEAD):
-            one_round(r)
         transpose_lora_b()
-        for r in range(-LORA_AHEAD, TILES + PROJECT_BEHIND):
+        for r in range(-PREPARE_AHEAD, TILES + PROJECT_BEHIND):
             one_round(r)

@@ -19,16 +19,15 @@ D = 512
 F = 512
 R = 128
 TILES = TOKENS // P
-GROUP = 4
-GROUPS = TILES // GROUP
+PAIR = 2
+PAIRS = TILES // PAIR
 LORA_SCALING = 2.0
+LOADS = (2, 2, 4, 4, 4, 4, 4, 4, 4)
 
-PREPARE_AHEAD = 4
-QUANTISE_AHEAD = 3
-LORA_AHEAD = 1
-GATE_BEHIND = 1
-TRANSPOSE_BEHIND = 4
-PROJECT_BEHIND = 6
+PREPARE_AHEAD = 2
+ROUND_BEHIND = 1
+TRANSPOSE_BEHIND = 2
+PROJECT_BEHIND = 3
 
 FLOPS = 2 * TOKENS * (2 * D * F + 2 * R * F + F * R)
 
@@ -59,10 +58,10 @@ def tile_feedforward_pa_t_kernel(
 
     with ExitStack() as ctx:
         consts = ctx.enter_context(tc.tile_pool(name="consts", bufs=1))
-        inputs = ctx.enter_context(tc.tile_pool(name="inputs", bufs=GROUPS))
-        ahead = ctx.enter_context(tc.tile_pool(name="ahead", bufs=6))
+        inputs = ctx.enter_context(tc.tile_pool(name="inputs", bufs=1))
+        ahead = ctx.enter_context(tc.tile_pool(name="ahead", bufs=4))
         work = ctx.enter_context(tc.tile_pool(name="work", bufs=3))
-        behind = ctx.enter_context(tc.tile_pool(name="behind", bufs=7))
+        behind = ctx.enter_context(tc.tile_pool(name="behind", bufs=4))
         banks = ctx.enter_context(tc.psum_pool(name="banks", bufs=1))
         ctx.enter_context(tc.manual_schedule())
 
@@ -82,18 +81,21 @@ def tile_feedforward_pa_t_kernel(
         for plane in (w1_plane, w3_plane, a2_plane):
             nc.vector.memset(plane[:].bitcast(I32), 0)
 
-        x_in = []
-        xa_in = []
+        x_in = {}
+        xa_in = {}
+        first_tiles = [sum(LOADS[:n]) for n in range(len(LOADS))]
 
-        def load_group(grp):
-            tiles = slice(grp * GROUP, (grp + 1) * GROUP)
-            x_g = inputs.tile([P, GROUP, D], BF16, name="x_g")
-            nc.sync.dma_start(out=x_g[:], in_=x_v[:, tiles, :])
-            xa_g = inputs.tile([P, 2, GROUP, R], BF16, name="xa_g")
-            nc.sync.dma_start(out=xa_g[:, 0], in_=xa1_v[:, tiles, :])
-            nc.sync.dma_start(out=xa_g[:, 1], in_=xa3_v[:, tiles, :])
-            x_in.append(x_g)
-            xa_in.append(xa_g)
+        def load_inputs(n, x_queue, xa_queue):
+            first, count = first_tiles[n], LOADS[n]
+            tiles = slice(first, first + count)
+            x_g = inputs.tile([P, count, D], BF16, name="x_g%d" % n)
+            x_queue.dma_start(out=x_g[:], in_=x_v[:, tiles, :])
+            xa_g = inputs.tile([P, 2, count, R], BF16, name="xa_g%d" % n)
+            xa_queue.dma_start(out=xa_g[:, 0], in_=xa1_v[:, tiles, :])
+            xa_queue.dma_start(out=xa_g[:, 1], in_=xa3_v[:, tiles, :])
+            for j in range(count):
+                x_in[first + j] = x_g[:, j, :]
+                xa_in[first + j] = (xa_g[:, 0, j, :], xa_g[:, 1, j, :])
 
         def load_scales(plane, scales):
             for quad in range(4):
@@ -115,30 +117,36 @@ def tile_feedforward_pa_t_kernel(
 
         nc.sync.dma_start(out=b_in[:, 0], in_=lora_B1.rearrange("(c p) r -> p c r", p=P))
         nc.sync.dma_start(out=b_in[:, 1], in_=lora_B3.rearrange("(c p) r -> p c r", p=P))
-        load_group(0)
+        load_inputs(0, nc.sync, nc.sync)
         load_words(w1_sb, w1_words)
-        load_words(w3_sb, w3_words)
         load_scales(w1_plane, w1_scales)
+        load_words(w3_sb, w3_words)
         load_scales(w3_plane, w3_scales)
-        load_group(1)
-        load_scales(a2_plane, lora_A2_scales)
+        load_inputs(1, nc.gpsimd, nc.gpsimd)
+        load_inputs(2, nc.sync, nc.sync)
         load_words(a2_sb, lora_A2_words)
-        for grp in range(2, GROUPS):
-            load_group(grp)
+        load_scales(a2_plane, lora_A2_scales)
+        for n in range(3, len(LOADS)):
+            load_inputs(n, nc.sync, nc.sync)
 
         x_grouped = {}
         x_codes = {}
         xaT = {}
+        lora_ps = {}
         lora_sb = {}
+        mx_ps = {}
         h_sb = {}
-        g_tiles = {}
+        s1 = {}
+        g_sb = {}
+        g_bf = {}
+        g_grouped = {}
         g_codes = {}
-        ga2_groups = {}
+        psum = {}
         bT = consts.tile([P, 2, F], BF16)
         weights = ((w1_sb, w1_plane), (w3_sb, w3_plane))
 
-        def live(i):
-            return 0 <= i < TILES
+        def live(q):
+            return 0 <= q < PAIRS
 
         def transpose_lora_b():
             bT_ps = banks.tile([P, 2, F], BF16, tag="gT_ps", name="bT_ps")
@@ -147,132 +155,216 @@ def tile_feedforward_pa_t_kernel(
                     nc.tensor.transpose(bT_ps[:, which, c * P : (c + 1) * P], b_in[:, which, c, :], ident_bf[:])
             nc.vector.tensor_copy(out=bT[:], in_=bT_ps[:])
 
-        def one_round(r):
-            prep = r + PREPARE_AHEAD
-            quant = r + QUANTISE_AHEAD
-            ahead_tile = r + LORA_AHEAD
-            gate = r - GATE_BEHIND
-            back = r - TRANSPOSE_BEHIND
-            proj = r - PROJECT_BEHIND
-
-            mx_ps = {}
-            lora_ps = {}
-
-            def lora_matmul(which):
+        def lora_matmuls(tile):
+            for which in range(2):
                 lora_ps[which] = banks.tile([P, F], F32, name="lora_ps%d" % which)
                 nc.tensor.matmul(
                     out=lora_ps[which][:],
-                    lhsT=xaT[ahead_tile][:, which, :],
+                    lhsT=xaT[tile // PAIR][:, tile % PAIR, which, :],
                     rhs=bT[:, which, :],
                     start=True,
                     stop=True,
                 )
 
-            if live(ahead_tile):
-                lora_matmul(0)
+        def mx_matmuls(tile):
+            words, plane = x_codes[tile // PAIR]
+            cols = slice(tile % PAIR * P, (tile % PAIR + 1) * P)
             for which in range(2):
-                if live(r):
-                    words, plane = x_codes[r]
-                    w_sb, w_plane = weights[which]
-                    mx_ps[which] = banks.tile([P, F], F32, name="mx_ps%d" % which)
-                    nc.tensor.matmul_mx(
-                        out=mx_ps[which][:],
-                        lhsT=words[:].bitcast(FP8X4),
-                        lhsT_scale=plane[:],
-                        rhs=w_sb[:].bitcast(FP8X4),
-                        rhs_scale=w_plane[:],
-                        start=True,
-                        stop=True,
-                    )
-            if live(proj):
-                words, plane = g_codes[proj]
-                ga2_ps = banks.tile([P, R], F32, name="ga2_ps")
+                w_sb, w_plane = weights[which]
+                mx_ps[which] = banks.tile([P, F], F32, name="mx_ps%d" % which)
                 nc.tensor.matmul_mx(
-                    out=ga2_ps[:],
-                    lhsT=words[:].bitcast(FP8X4),
-                    lhsT_scale=plane[:],
+                    out=mx_ps[which][:],
+                    lhsT=words[:, cols].bitcast(FP8X4),
+                    lhsT_scale=plane[:, cols],
+                    rhs=w_sb[:].bitcast(FP8X4),
+                    rhs_scale=w_plane[:],
+                    start=True,
+                    stop=True,
+                )
+
+        def project(q):
+            words, plane = g_codes[q]
+            psum["ga2"] = banks.tile([P, PAIR, R], F32, name="ga2_ps")
+            for i in range(PAIR):
+                cols = slice(i * P, (i + 1) * P)
+                nc.tensor.matmul_mx(
+                    out=psum["ga2"][:, i, :],
+                    lhsT=words[:, cols].bitcast(FP8X4),
+                    lhsT_scale=plane[:, cols],
                     rhs=a2_sb[:].bitcast(FP8X4),
                     rhs_scale=a2_plane[:],
                     start=True,
                     stop=True,
                 )
-            if live(ahead_tile):
-                lora_matmul(1)
-            if live(back):
-                gT_ps = banks.tile([P, PACK, P], F32, name="gT_ps")
-                for t in range(PACK):
-                    nc.tensor.transpose(gT_ps[:, t, :], g_tiles[back][:, t:F:PACK], ident_f32[:])
-            if live(prep):
-                x_words = x_in[prep // GROUP][:, prep % GROUP, :].bitcast(F32)
-                xT_ps = banks.tile([P, 2, P], F32, name="xT_ps")
+
+        def transpose_g(q):
+            gT_ps = banks.tile([P, PAIR, 2, P], F32, name="gT_ps")
+            g_words = g_bf[q][:].bitcast(F32).rearrange("q (u i p) -> q u i p", u=2, i=PAIR)
+            for i in range(PAIR):
                 for u in range(2):
-                    nc.tensor.transpose(xT_ps[:, u, :], x_words[:, u : D // 2 : 2], ident_f32[:])
-                xaT_ps = banks.tile([P, 2, P], BF16, name="xaT_ps")
-                for which in range(2):
-                    nc.tensor.transpose(xaT_ps[:, which, :], xa_in[prep // GROUP][:, which, prep % GROUP, :], ident_bf[:])
+                    nc.tensor.transpose(gT_ps[:, i, u, :], g_words[:, u, i, :], ident_f32[:])
+            psum["gT"] = gT_ps
 
-            if live(gate):
-                s1 = work.tile([P, F], F32, name="s1")
-                nc.scalar.activation(out=s1[:], in_=h_sb[gate][0][:], func=ACT.Silu)
-            if live(ahead_tile):
-                lora_sb[ahead_tile] = []
+        def transpose_inputs(q):
+            xT_ps = banks.tile([P, PAIR, 2, P], F32, name="xT_ps")
+            xaT_ps = banks.tile([P, PAIR, 2, P], BF16, name="xaT_ps")
+            for i in range(PAIR):
+                x_words = x_in[q * PAIR + i].bitcast(F32)
+                for u in range(2):
+                    nc.tensor.transpose(xT_ps[:, i, u, :], x_words[:, u : D // 2 : 2], ident_f32[:])
+            for i in range(PAIR):
                 for which in range(2):
-                    copy_sb = work.tile([P, F], F32, name="lora_sb%d" % which)
-                    nc.scalar.copy(out=copy_sb[:], in_=lora_ps[which][:])
-                    lora_sb[ahead_tile].append(copy_sb)
-            if live(proj):
-                if proj % GROUP == 0:
-                    ga2_groups["sb"] = behind.tile([P, GROUP, R], F32, name="ga2_sb", bufs=2)
-                nc.scalar.copy(out=ga2_groups["sb"][:, proj % GROUP, :], in_=ga2_ps[:])
-                if proj % GROUP == GROUP - 1:
-                    nc.sync.dma_start(out=ga2_v[:, proj - GROUP + 1 : proj + 1, :], in_=ga2_groups["sb"][:])
-            if live(prep):
-                grouped = ahead.tile([P, P * PACK], BF16, align_bytes=64, name="x_grouped")
-                nc.scalar.copy(
-                    out=grouped[:].bitcast(F32).rearrange("p (r u) -> p r u", u=2),
-                    in_=xT_ps[:].rearrange("p u r -> p r u"),
+                    nc.tensor.transpose(xaT_ps[:, i, which, :], xa_in[q * PAIR + i][which], ident_bf[:])
+            psum["xT"] = xT_ps
+            psum["xaT"] = xaT_ps
+
+        def copy_lora(tile):
+            lora_sb[tile] = []
+            for which in range(2):
+                copy_sb = work.tile([P, F], F32, name="lora_sb%d" % which)
+                nc.scalar.copy(out=copy_sb[:], in_=lora_ps[which][:])
+                lora_sb[tile].append(copy_sb)
+
+        def copy_projection(q):
+            ga2_sb = behind.tile([P, PAIR, R], F32, name="ga2_sb")
+            nc.scalar.copy(out=ga2_sb[:], in_=psum["ga2"][:])
+            nc.sync.dma_start(out=ga2_v[:, q * PAIR : (q + 1) * PAIR, :], in_=ga2_sb[:])
+
+        def copy_x(q):
+            grouped = ahead.tile([P, PAIR * P * PACK], BF16, align_bytes=64, name="x_grouped")
+            nc.scalar.copy(
+                out=grouped[:].bitcast(F32).rearrange("p (i r u) -> p i r u", i=PAIR, u=2),
+                in_=psum["xT"][:].rearrange("p i u r -> p i r u"),
+            )
+            x_grouped[q] = grouped
+
+        def gate(q, tiles):
+            if q not in s1:
+                s1[q] = work.tile([P, PAIR, F], F32, name="s1")
+            nc.scalar.activation(out=s1[q][:, tiles, :], in_=h_sb[q][0][:, tiles, :], func=ACT.Silu)
+
+        def multiply(engine, q, tiles):
+            if q not in g_sb:
+                g_sb[q] = behind.tile([P, PAIR, F], F32, name="g_sb")
+            engine.tensor_tensor(out=g_sb[q][:, tiles, :], in0=s1[q][:, tiles, :], in1=h_sb[q][1][:, tiles, :], op=ALU.mult)
+            nc.sync.dma_start(
+                out=g_v[:, q * PAIR + tiles.start : q * PAIR + tiles.stop, :], in_=g_sb[q][:, tiles, :]
+            )
+
+        def add_lora(tile):
+            q, i = tile // PAIR, tile % PAIR
+            if i == 0:
+                h_sb[q] = [work.tile([P, PAIR, F], F32, name="h%d" % which) for which in range(2)]
+            for which in range(2):
+                nc.vector.scalar_tensor_tensor(
+                    out=h_sb[q][which][:, i, :],
+                    in0=lora_sb[tile][which][:],
+                    scalar=LORA_SCALING,
+                    in1=mx_ps[which][:],
+                    op0=ALU.mult,
+                    op1=ALU.add,
                 )
-                x_grouped[prep] = grouped
 
-            if live(gate):
-                g_sb = behind.tile([P, F], F32, name="g_sb")
-                nc.gpsimd.tensor_tensor(out=g_sb[:], in0=s1[:], in1=h_sb[gate][1][:], op=ALU.mult)
-                nc.sync.dma_start(out=g_v[:, gate, :], in_=g_sb[:])
-                g_tiles[gate] = g_sb
+        def copy_gT(q, copy):
+            g_grouped[q] = behind.tile([P, PAIR * P * PACK], BF16, align_bytes=64, name="g_grouped")
+            copy(
+                out=g_grouped[q][:].bitcast(F32).rearrange("p (i r u) -> p i r u", i=PAIR, u=2),
+                in_=psum["gT"][:].rearrange("p i u r -> p i r u"),
+            )
+
+        def copy_xaT(q):
+            xaT[q] = ahead.tile([P, PAIR, 2, P], BF16, name="xaT_sb")
+            nc.vector.tensor_copy(out=xaT[q][:], in_=psum["xaT"][:])
+
+        def round_g(q):
+            g_bf[q] = behind.tile([P, PAIR * F], BF16, name="g_bf")
+            nc.vector.tensor_copy(
+                out=g_bf[q][:].rearrange("q (u n e) -> q u n e", u=2, e=2),
+                in_=g_sb[q][:].rearrange("q i (p u e) -> q u (i p) e", u=2, e=2),
+            )
+
+        def quantise(source, pool, name):
+            words = pool.tile([P, PAIR * P], U32, align_bytes=64, name=name + "_words")
+            plane = pool.tile([P, PAIR * P], U8, align_bytes=64, name=name + "_plane")
+            nc.vector.quantize_mx(out=words[:].bitcast(FP8X4), scales=plane[:], in_=source[:])
+            return words, plane
+
+        both = slice(0, PAIR)
+        singly = [slice(i, i + 1) for i in range(PAIR)]
+
+        def prepare(q):
+            transpose_inputs(q)
+            copy_x(q)
+            copy_xaT(q)
+
+        def quantise_x(q):
+            x_codes[q] = quantise(x_grouped[q], ahead, "xq")
+
+        def lora(tile):
+            lora_matmuls(tile)
+            copy_lora(tile)
+
+        def mx(tile):
+            mx_matmuls(tile)
+            add_lora(tile)
+
+        def first_round():
+            transpose_lora_b()
+            prepare(0)
+            quantise_x(0)
+            for tile in range(PAIR):
+                lora(tile)
+                mx(tile)
+            prepare(1)
+            gate(0, both)
+            quantise_x(1)
+            multiply(nc.gpsimd, 0, both)
+            lora(PAIR)
+            prepare(2)
+            quantise_x(2)
+
+        def one_round(r):
+            prep = r + PREPARE_AHEAD
+            rnd = r - ROUND_BEHIND
+            back = r - TRANSPOSE_BEHIND
+            proj = r - PROJECT_BEHIND
+            a, b = r * PAIR, r * PAIR + 1
+            last = r == PAIRS - 1
 
             if live(r):
-                h_sb[r] = []
-                for which in range(2):
-                    h = work.tile([P, F], F32, name="h%d" % which, bufs=4)
-                    nc.vector.scalar_tensor_tensor(
-                        out=h[:],
-                        in0=lora_sb[r][which][:],
-                        scalar=LORA_SCALING,
-                        in1=mx_ps[which][:],
-                        op0=ALU.mult,
-                        op1=ALU.add,
-                    )
-                    h_sb[r].append(h)
+                lora(b)
+                mx(a)
+            if last:
+                gate(r, singly[0])
             if live(back):
-                g_grouped = behind.tile([P, P, PACK], BF16, align_bytes=64, name="g_grouped")
-                nc.vector.tensor_copy(out=g_grouped[:], in_=gT_ps[:].rearrange("p t r -> p r t"))
-            if live(quant):
-                words = ahead.tile([P, P], U32, align_bytes=64, name="x_words_q")
-                plane = ahead.tile([P, P], U8, align_bytes=64, name="x_plane_q")
-                nc.vector.quantize_mx(out=words[:].bitcast(FP8X4), scales=plane[:], in_=x_grouped[quant][:])
-                x_codes[quant] = (words, plane)
+                transpose_g(back)
+                copy_gT(back, nc.vector.tensor_copy if live(r + 1) else nc.scalar.copy)
             if live(prep):
-                xaT_new = ahead.tile([P, 2, P], BF16, name="xaT_sb")
-                nc.vector.tensor_copy(out=xaT_new[:], in_=xaT_ps[:])
-                xaT[prep] = xaT_new
+                prepare(prep)
+            if live(r + 1):
+                lora(a + PAIR)
+            if live(r):
+                mx(b)
+            if live(proj):
+                project(proj)
+            if last:
+                gate(r, singly[1])
+            elif live(r):
+                gate(r, both)
+            if live(proj):
+                copy_projection(proj)
+            if live(rnd):
+                round_g(rnd)
+            if last:
+                for tiles in singly:
+                    multiply(nc.vector, r, tiles)
+            if live(prep):
+                quantise_x(prep)
             if live(back):
-                words = behind.tile([P, P], U32, align_bytes=64, name="g_words_q")
-                plane = behind.tile([P, P], U8, align_bytes=64, name="g_plane_q")
-                nc.vector.quantize_mx(
-                    out=words[:].bitcast(FP8X4), scales=plane[:], in_=g_grouped[:].rearrange("p r t -> p (r t)")
-                )
-                g_codes[back] = (words, plane)
+                g_codes[back] = quantise(g_grouped[back], behind, "gq")
+            if live(r) and not last:
+                multiply(nc.gpsimd, r, both)
 
-        transpose_lora_b()
-        for r in range(-PREPARE_AHEAD, TILES + PROJECT_BEHIND):
+        first_round()
+        for r in range(1, PAIRS + PROJECT_BEHIND):
             one_round(r)

@@ -22,7 +22,7 @@ TILES = TOKENS // P
 PAIR = 2
 PAIRS = TILES // PAIR
 LORA_SCALING = 2.0
-LOADS = (2, 2, 4, 4, 4, 4, 4, 4, 4)
+LOADS = (2, 4, 4, 4, 4, 4, 4, 4, 2)
 
 PREPARE_AHEAD = 2
 ROUND_BEHIND = 1
@@ -66,9 +66,7 @@ def tile_feedforward_pa_t_kernel(
         ctx.enter_context(tc.manual_schedule())
 
         ident_bf = consts.tile([P, P], BF16)
-        make_identity(nc, ident_bf[:])
         ident_f32 = consts.tile([P, P], F32)
-        make_identity(nc, ident_f32[:])
 
         warm_in = consts.tile([P, 1], F32)
         warm_out = consts.tile([P, 1], F32)
@@ -117,11 +115,13 @@ def tile_feedforward_pa_t_kernel(
 
         nc.sync.dma_start(out=b_in[:, 0], in_=lora_B1.rearrange("(c p) r -> p c r", p=P))
         nc.sync.dma_start(out=b_in[:, 1], in_=lora_B3.rearrange("(c p) r -> p c r", p=P))
-        load_inputs(0, nc.sync, nc.sync)
+        load_inputs(0, nc.sync, nc.gpsimd)
         load_words(w1_sb, w1_words)
         load_scales(w1_plane, w1_scales)
         load_words(w3_sb, w3_words)
         load_scales(w3_plane, w3_scales)
+        make_identity(nc, ident_bf[:])
+        make_identity(nc, ident_f32[:])
         load_inputs(1, nc.gpsimd, nc.gpsimd)
         load_inputs(2, nc.sync, nc.sync)
         load_words(a2_sb, lora_A2_words)
@@ -148,43 +148,40 @@ def tile_feedforward_pa_t_kernel(
         def live(q):
             return 0 <= q < PAIRS
 
-        def transpose_lora_b():
-            bT_ps = banks.tile([P, 2, F], BF16, tag="gT_ps", name="bT_ps")
-            for which in range(2):
-                for c in range(F // P):
-                    nc.tensor.transpose(bT_ps[:, which, c * P : (c + 1) * P], b_in[:, which, c, :], ident_bf[:])
-            nc.vector.tensor_copy(out=bT[:], in_=bT_ps[:])
+        def transpose_lora_b(which, tag, nbanks, copy):
+            bT_ps = banks.tile([P, F], BF16, tag=tag, name="bT_ps", bufs=nbanks)
+            for c in range(F // P):
+                nc.tensor.transpose(bT_ps[:, c * P : (c + 1) * P], b_in[:, which, c, :], ident_bf[:])
+            copy(out=bT[:, which, :], in_=bT_ps[:])
 
-        def lora_matmuls(tile):
-            for which in range(2):
-                lora_ps[which] = banks.tile([P, F], F32, name="lora_ps%d" % which)
-                nc.tensor.matmul(
-                    out=lora_ps[which][:],
-                    lhsT=xaT[tile // PAIR][:, tile % PAIR, which, :],
-                    rhs=bT[:, which, :],
-                    start=True,
-                    stop=True,
-                )
+        def lora_matmul(tile, which):
+            lora_ps[tile, which] = banks.tile([P, F], F32, name="lora_ps", bufs=2)
+            nc.tensor.matmul(
+                out=lora_ps[tile, which][:],
+                lhsT=xaT[tile // PAIR][:, tile % PAIR, which, :],
+                rhs=bT[:, which, :],
+                start=True,
+                stop=True,
+            )
 
-        def mx_matmuls(tile):
+        def mx_matmul(tile, which):
             words, plane = x_codes[tile // PAIR]
             cols = slice(tile % PAIR * P, (tile % PAIR + 1) * P)
-            for which in range(2):
-                w_sb, w_plane = weights[which]
-                mx_ps[which] = banks.tile([P, F], F32, name="mx_ps%d" % which)
-                nc.tensor.matmul_mx(
-                    out=mx_ps[which][:],
-                    lhsT=words[:, cols].bitcast(FP8X4),
-                    lhsT_scale=plane[:, cols],
-                    rhs=w_sb[:].bitcast(FP8X4),
-                    rhs_scale=w_plane[:],
-                    start=True,
-                    stop=True,
-                )
+            w_sb, w_plane = weights[which]
+            mx_ps[tile, which] = banks.tile([P, F], F32, name="mx_ps", bufs=2)
+            nc.tensor.matmul_mx(
+                out=mx_ps[tile, which][:],
+                lhsT=words[:, cols].bitcast(FP8X4),
+                lhsT_scale=plane[:, cols],
+                rhs=w_sb[:].bitcast(FP8X4),
+                rhs_scale=w_plane[:],
+                start=True,
+                stop=True,
+            )
 
         def project(q):
             words, plane = g_codes[q]
-            psum["ga2"] = banks.tile([P, PAIR, R], F32, name="ga2_ps")
+            psum["ga2"] = banks.tile([P, PAIR, R], F32, tag="ga2_ps", name="ga2_ps", bufs=1)
             for i in range(PAIR):
                 cols = slice(i * P, (i + 1) * P)
                 nc.tensor.matmul_mx(
@@ -198,7 +195,7 @@ def tile_feedforward_pa_t_kernel(
                 )
 
         def transpose_g(q):
-            gT_ps = banks.tile([P, PAIR, 2, P], F32, name="gT_ps")
+            gT_ps = banks.tile([P, PAIR, 2, P], F32, tag="gT_ps", name="gT_ps", bufs=1)
             g_words = g_bf[q][:].bitcast(F32).rearrange("q (u i p) -> q u i p", u=2, i=PAIR)
             for i in range(PAIR):
                 for u in range(2):
@@ -206,33 +203,36 @@ def tile_feedforward_pa_t_kernel(
             psum["gT"] = gT_ps
 
         def transpose_inputs(q):
-            xT_ps = banks.tile([P, PAIR, 2, P], F32, name="xT_ps")
-            xaT_ps = banks.tile([P, PAIR, 2, P], BF16, name="xaT_ps")
+            transpose_x(q)
+            transpose_xa(q)
+
+        def transpose_x(q):
+            xT_ps = banks.tile([P, PAIR, 2, P], F32, tag="xT_ps", name="xT_ps", bufs=1)
+            psum["xT"] = xT_ps
             for i in range(PAIR):
                 x_words = x_in[q * PAIR + i].bitcast(F32)
                 for u in range(2):
                     nc.tensor.transpose(xT_ps[:, i, u, :], x_words[:, u : D // 2 : 2], ident_f32[:])
+
+        def transpose_xa(q):
+            xaT_ps = banks.tile([P, PAIR, 2, P], BF16, tag="xaT_ps", name="xaT_ps", bufs=1)
+            psum["xaT"] = xaT_ps
             for i in range(PAIR):
                 for which in range(2):
                     nc.tensor.transpose(xaT_ps[:, i, which, :], xa_in[q * PAIR + i][which], ident_bf[:])
-            psum["xT"] = xT_ps
-            psum["xaT"] = xaT_ps
 
-        def copy_lora(tile):
-            lora_sb[tile] = []
-            for which in range(2):
-                copy_sb = work.tile([P, F], F32, name="lora_sb%d" % which)
-                nc.scalar.copy(out=copy_sb[:], in_=lora_ps[which][:])
-                lora_sb[tile].append(copy_sb)
+        def copy_lora(tile, which):
+            lora_sb[tile, which] = work.tile([P, F], F32, name="lora_sb%d" % which)
+            nc.scalar.copy(out=lora_sb[tile, which][:], in_=lora_ps[tile, which][:])
 
-        def copy_projection(q):
+        def copy_projection(q, copy):
             ga2_sb = behind.tile([P, PAIR, R], F32, name="ga2_sb")
-            nc.scalar.copy(out=ga2_sb[:], in_=psum["ga2"][:])
+            copy(out=ga2_sb[:], in_=psum["ga2"][:])
             nc.sync.dma_start(out=ga2_v[:, q * PAIR : (q + 1) * PAIR, :], in_=ga2_sb[:])
 
-        def copy_x(q):
+        def copy_x(q, copy):
             grouped = ahead.tile([P, PAIR * P * PACK], BF16, align_bytes=64, name="x_grouped")
-            nc.scalar.copy(
+            copy(
                 out=grouped[:].bitcast(F32).rearrange("p (i r u) -> p i r u", i=PAIR, u=2),
                 in_=psum["xT"][:].rearrange("p i u r -> p i r u"),
             )
@@ -251,19 +251,18 @@ def tile_feedforward_pa_t_kernel(
                 out=g_v[:, q * PAIR + tiles.start : q * PAIR + tiles.stop, :], in_=g_sb[q][:, tiles, :]
             )
 
-        def add_lora(tile):
+        def add_lora(tile, which):
             q, i = tile // PAIR, tile % PAIR
-            if i == 0:
-                h_sb[q] = [work.tile([P, PAIR, F], F32, name="h%d" % which) for which in range(2)]
-            for which in range(2):
-                nc.vector.scalar_tensor_tensor(
-                    out=h_sb[q][which][:, i, :],
-                    in0=lora_sb[tile][which][:],
-                    scalar=LORA_SCALING,
-                    in1=mx_ps[which][:],
-                    op0=ALU.mult,
-                    op1=ALU.add,
-                )
+            if q not in h_sb:
+                h_sb[q] = [work.tile([P, PAIR, F], F32, name="h%d" % w) for w in range(2)]
+            nc.vector.scalar_tensor_tensor(
+                out=h_sb[q][which][:, i, :],
+                in0=lora_sb[tile, which][:],
+                scalar=LORA_SCALING,
+                in1=mx_ps[tile, which][:],
+                op0=ALU.mult,
+                op1=ALU.add,
+            )
 
         def copy_gT(q, copy):
             g_grouped[q] = behind.tile([P, PAIR * P * PACK], BF16, align_bytes=64, name="g_grouped")
@@ -272,9 +271,9 @@ def tile_feedforward_pa_t_kernel(
                 in_=psum["gT"][:].rearrange("p i u r -> p i r u"),
             )
 
-        def copy_xaT(q):
+        def copy_xaT(q, copy):
             xaT[q] = ahead.tile([P, PAIR, 2, P], BF16, name="xaT_sb")
-            nc.vector.tensor_copy(out=xaT[q][:], in_=psum["xaT"][:])
+            copy(out=xaT[q][:], in_=psum["xaT"][:])
 
         def round_g(q):
             g_bf[q] = behind.tile([P, PAIR * F], BF16, name="g_bf")
@@ -292,36 +291,62 @@ def tile_feedforward_pa_t_kernel(
         both = slice(0, PAIR)
         singly = [slice(i, i + 1) for i in range(PAIR)]
 
-        def prepare(q):
-            transpose_inputs(q)
-            copy_x(q)
-            copy_xaT(q)
-
         def quantise_x(q):
             x_codes[q] = quantise(x_grouped[q], ahead, "xq")
 
         def lora(tile):
-            lora_matmuls(tile)
-            copy_lora(tile)
+            for which in range(2):
+                lora_matmul(tile, which)
+                copy_lora(tile, which)
 
         def mx(tile):
-            mx_matmuls(tile)
-            add_lora(tile)
+            for which in range(2):
+                mx_matmul(tile, which)
+                add_lora(tile, which)
+
+        def prepare(q):
+            transpose_inputs(q)
+            copy_x(q, nc.scalar.copy)
+            copy_xaT(q, nc.vector.tensor_copy)
 
         def first_round():
-            transpose_lora_b()
-            prepare(0)
+            transpose_lora_b(0, "gT_ps", 1, nc.vector.tensor_copy)
+            transpose_lora_b(1, "ga2_ps", 1, nc.scalar.copy)
+            transpose_xa(0)
+            copy_xaT(0, nc.vector.tensor_copy)
+            transpose_x(0)
+            copy_x(0, nc.scalar.copy)
             quantise_x(0)
-            for tile in range(PAIR):
-                lora(tile)
-                mx(tile)
-            prepare(1)
-            gate(0, both)
+            lora(0)
+            lora_matmul(1, 0)
+            mx_matmul(0, 0)
+            lora_matmul(1, 1)
+            mx_matmul(0, 1)
+            add_lora(0, 0)
+            add_lora(0, 1)
+            copy_lora(1, 0)
+            copy_lora(1, 1)
+            transpose_inputs(1)
+            copy_x(1, nc.scalar.copy)
+            mx_matmul(1, 0)
+            mx_matmul(1, 1)
+            copy_xaT(1, nc.vector.tensor_copy)
+            add_lora(1, 0)
+            add_lora(1, 1)
             quantise_x(1)
+            lora_matmul(2, 0)
+            lora_matmul(2, 1)
+            transpose_inputs(2)
+            copy_lora(2, 0)
+            gate(0, both)
+            copy_lora(2, 1)
+            copy_x(2, nc.scalar.copy)
+            copy_xaT(2, nc.vector.tensor_copy)
+            lora_matmul(3, 0)
+            mx_matmul(2, 0)
+            lora_matmul(3, 1)
+            mx_matmul(2, 1)
             multiply(nc.gpsimd, 0, both)
-            lora(PAIR)
-            prepare(2)
-            quantise_x(2)
 
         def one_round(r):
             prep = r + PREPARE_AHEAD
@@ -330,34 +355,62 @@ def tile_feedforward_pa_t_kernel(
             proj = r - PROJECT_BEHIND
             a, b = r * PAIR, r * PAIR + 1
             last = r == PAIRS - 1
-
+            if live(back):
+                transpose_g(back)
+            if live(prep):
+                transpose_inputs(prep)
             if live(r):
-                lora(b)
-                mx(a)
+                add_lora(a, 0)
+            if live(r):
+                add_lora(a, 1)
+            if r == 1:
+                quantise_x(2)
+            if live(r):
+                copy_lora(b, 0)
+            if live(r):
+                copy_lora(b, 1)
             if last:
                 gate(r, singly[0])
             if live(back):
-                transpose_g(back)
                 copy_gT(back, nc.vector.tensor_copy if live(r + 1) else nc.scalar.copy)
             if live(prep):
-                prepare(prep)
-            if live(r + 1):
-                lora(a + PAIR)
+                copy_x(prep, nc.scalar.copy)
+            if live(prep):
+                copy_xaT(prep, nc.vector.tensor_copy)
             if live(r):
-                mx(b)
+                mx_matmul(b, 0)
+            if live(r + 1):
+                lora_matmul(a + PAIR, 0)
+            if live(r + 1):
+                lora_matmul(a + PAIR, 1)
+            if live(r):
+                mx_matmul(b, 1)
             if live(proj):
                 project(proj)
-            if last:
-                gate(r, singly[1])
-            elif live(r):
-                gate(r, both)
+            if live(r + 1):
+                copy_lora(a + PAIR, 0)
+            if live(r + 1):
+                copy_lora(a + PAIR, 1)
+            if live(r):
+                add_lora(b, 0)
+            if live(r):
+                add_lora(b, 1)
+            if live(r):
+                gate(r, singly[1] if last else both)
             if live(proj):
-                copy_projection(proj)
+                copy_projection(proj, nc.scalar.copy)
+            if live(r + 1):
+                lora_matmul(b + PAIR, 0)
+            if live(r + 1):
+                mx_matmul(a + PAIR, 0)
+            if live(r + 1):
+                lora_matmul(b + PAIR, 1)
+            if live(r + 1):
+                mx_matmul(a + PAIR, 1)
             if live(rnd):
                 round_g(rnd)
             if last:
-                for tiles in singly:
-                    multiply(nc.vector, r, tiles)
+                for tiles in singly: multiply(nc.vector, r, tiles)
             if live(prep):
                 quantise_x(prep)
             if live(back):

@@ -22,7 +22,7 @@ TILES = TOKENS // P
 PAIR = 2
 PAIRS = TILES // PAIR
 LORA_SCALING = 2.0
-LOADS = (2, 4, 4, 4, 4, 4, 4, 4, 2)
+LOADS = (2, 2, 4, 4, 4, 4, 4, 4, 4)
 
 PREPARE_AHEAD = 2
 ROUND_BEHIND = 1
@@ -66,7 +66,9 @@ def tile_feedforward_pa_t_kernel(
         ctx.enter_context(tc.manual_schedule())
 
         ident_bf = consts.tile([P, P], BF16)
+        make_identity(nc, ident_bf[:])
         ident_f32 = consts.tile([P, P], F32)
+        make_identity(nc, ident_f32[:])
 
         warm_in = consts.tile([P, 1], F32)
         warm_out = consts.tile([P, 1], F32)
@@ -115,14 +117,12 @@ def tile_feedforward_pa_t_kernel(
 
         nc.sync.dma_start(out=b_in[:, 0], in_=lora_B1.rearrange("(c p) r -> p c r", p=P))
         nc.sync.dma_start(out=b_in[:, 1], in_=lora_B3.rearrange("(c p) r -> p c r", p=P))
-        load_inputs(0, nc.sync, nc.gpsimd)
+        load_inputs(0, nc.sync, nc.sync)
         load_words(w1_sb, w1_words)
         load_scales(w1_plane, w1_scales)
         load_words(w3_sb, w3_words)
         load_scales(w3_plane, w3_scales)
-        make_identity(nc, ident_bf[:])
-        make_identity(nc, ident_f32[:])
-        load_inputs(1, nc.gpsimd, nc.gpsimd)
+        load_inputs(1, nc.sync, nc.sync)
         load_inputs(2, nc.sync, nc.sync)
         load_words(a2_sb, lora_A2_words)
         load_scales(a2_plane, lora_A2_scales)
@@ -144,6 +144,8 @@ def tile_feedforward_pa_t_kernel(
         psum = {}
         bT = consts.tile([P, 2, F], BF16)
         weights = ((w1_sb, w1_plane), (w3_sb, w3_plane))
+        both = slice(0, PAIR)
+        singly = [slice(i, i + 1) for i in range(PAIR)]
 
         def live(q):
             return 0 <= q < PAIRS
@@ -179,10 +181,10 @@ def tile_feedforward_pa_t_kernel(
                 stop=True,
             )
 
-        def project(q):
+        def project(q, tiles=both, tag="ga2_ps", count=1):
             words, plane = g_codes[q]
-            psum["ga2"] = banks.tile([P, PAIR, R], F32, tag="ga2_ps", name="ga2_ps", bufs=1)
-            for i in range(PAIR):
+            psum["ga2"] = banks.tile([P, PAIR, R], F32, tag=tag, name="ga2_ps", bufs=count)
+            for i in range(tiles.start, tiles.stop):
                 cols = slice(i * P, (i + 1) * P)
                 nc.tensor.matmul_mx(
                     out=psum["ga2"][:, i, :],
@@ -194,10 +196,10 @@ def tile_feedforward_pa_t_kernel(
                     stop=True,
                 )
 
-        def transpose_g(q):
-            gT_ps = banks.tile([P, PAIR, 2, P], F32, tag="gT_ps", name="gT_ps", bufs=1)
+        def transpose_g(q, tiles=both, tag="gT_ps"):
+            gT_ps = banks.tile([P, PAIR, 2, P], F32, tag=tag, name="gT_ps", bufs=1)
             g_words = g_bf[q][:].bitcast(F32).rearrange("q (u i p) -> q u i p", u=2, i=PAIR)
-            for i in range(PAIR):
+            for i in range(tiles.start, tiles.stop):
                 for u in range(2):
                     nc.tensor.transpose(gT_ps[:, i, u, :], g_words[:, u, i, :], ident_f32[:])
             psum["gT"] = gT_ps
@@ -225,10 +227,12 @@ def tile_feedforward_pa_t_kernel(
             lora_sb[tile, which] = work.tile([P, F], F32, name="lora_sb%d" % which)
             nc.scalar.copy(out=lora_sb[tile, which][:], in_=lora_ps[tile, which][:])
 
-        def copy_projection(q, copy):
+        def copy_projection(q, copy, tiles=both):
             ga2_sb = behind.tile([P, PAIR, R], F32, name="ga2_sb")
-            copy(out=ga2_sb[:], in_=psum["ga2"][:])
-            nc.sync.dma_start(out=ga2_v[:, q * PAIR : (q + 1) * PAIR, :], in_=ga2_sb[:])
+            copy(out=ga2_sb[:, tiles, :], in_=psum["ga2"][:, tiles, :])
+            nc.sync.dma_start(
+                out=ga2_v[:, q * PAIR + tiles.start : q * PAIR + tiles.stop, :], in_=ga2_sb[:, tiles, :]
+            )
 
         def copy_x(q, copy):
             grouped = ahead.tile([P, PAIR * P * PACK], BF16, align_bytes=64, name="x_grouped")
@@ -264,50 +268,57 @@ def tile_feedforward_pa_t_kernel(
                 op1=ALU.add,
             )
 
-        def copy_gT(q, copy):
-            g_grouped[q] = behind.tile([P, PAIR * P * PACK], BF16, align_bytes=64, name="g_grouped")
+        def copy_gT(q, copy, tiles=both):
+            if q not in g_grouped:
+                g_grouped[q] = behind.tile([P, PAIR * P * PACK], BF16, align_bytes=64, name="g_grouped")
+            grouped_words = g_grouped[q][:].bitcast(F32).rearrange("p (i r u) -> p i r u", i=PAIR, u=2)
             copy(
-                out=g_grouped[q][:].bitcast(F32).rearrange("p (i r u) -> p i r u", i=PAIR, u=2),
-                in_=psum["gT"][:].rearrange("p i u r -> p i r u"),
+                out=grouped_words[:, tiles],
+                in_=psum["gT"][:].rearrange("p i u r -> p i r u")[:, tiles],
             )
 
         def copy_xaT(q, copy):
             xaT[q] = ahead.tile([P, PAIR, 2, P], BF16, name="xaT_sb")
             copy(out=xaT[q][:], in_=psum["xaT"][:])
 
-        def round_g(q):
-            g_bf[q] = behind.tile([P, PAIR * F], BF16, name="g_bf")
-            nc.vector.tensor_copy(
-                out=g_bf[q][:].rearrange("q (u n e) -> q u n e", u=2, e=2),
-                in_=g_sb[q][:].rearrange("q i (p u e) -> q u (i p) e", u=2, e=2),
+        def round_g(q, copy, tiles=both):
+            if q not in g_bf:
+                g_bf[q] = behind.tile([P, PAIR * F], BF16, name="g_bf")
+            ordered = g_bf[q][:].rearrange("q (u i n e) -> q u i n e", u=2, i=PAIR, e=2)[:, :, tiles]
+            copy(
+                out=ordered.rearrange("q u i n e -> q u (i n) e"),
+                in_=g_sb[q][:, tiles, :].rearrange("q i (n u e) -> q u (i n) e", u=2, e=2),
             )
 
-        def quantise(source, pool, name):
-            words = pool.tile([P, PAIR * P], U32, align_bytes=64, name=name + "_words")
-            plane = pool.tile([P, PAIR * P], U8, align_bytes=64, name=name + "_plane")
-            nc.vector.quantize_mx(out=words[:].bitcast(FP8X4), scales=plane[:], in_=source[:])
-            return words, plane
-
-        both = slice(0, PAIR)
-        singly = [slice(i, i + 1) for i in range(PAIR)]
+        def quantise(source, codes, tiles):
+            words, plane = codes
+            cols = slice(tiles.start * P, tiles.stop * P)
+            nc.vector.quantize_mx(
+                out=words[:, cols].bitcast(FP8X4),
+                scales=plane[:, cols],
+                in_=source[:, tiles.start * P * PACK : tiles.stop * P * PACK],
+            )
 
         def quantise_x(q):
-            x_codes[q] = quantise(x_grouped[q], ahead, "xq")
+            x_codes[q] = (
+                ahead.tile([P, PAIR * P], U32, align_bytes=64, name="xq_words"),
+                ahead.tile([P, PAIR * P], U8, align_bytes=64, name="xq_plane"),
+            )
+            quantise(x_grouped[q], x_codes[q], both)
+
+        def quantise_g(q, tiles=both):
+            if q not in g_codes:
+                g_codes[q] = (
+                    behind.tile([P, PAIR * P], U32, align_bytes=64, name="gq_words"),
+                    behind.tile([P, PAIR * P], U8, align_bytes=64, name="gq_plane"),
+                )
+            quantise(g_grouped[q], g_codes[q], tiles)
+
 
         def lora(tile):
             for which in range(2):
                 lora_matmul(tile, which)
                 copy_lora(tile, which)
-
-        def mx(tile):
-            for which in range(2):
-                mx_matmul(tile, which)
-                add_lora(tile, which)
-
-        def prepare(q):
-            transpose_inputs(q)
-            copy_x(q, nc.scalar.copy)
-            copy_xaT(q, nc.vector.tensor_copy)
 
         def first_round():
             transpose_lora_b(0, "gT_ps", 1, nc.vector.tensor_copy)
@@ -354,70 +365,83 @@ def tile_feedforward_pa_t_kernel(
             back = r - TRANSPOSE_BEHIND
             proj = r - PROJECT_BEHIND
             a, b = r * PAIR, r * PAIR + 1
-            last = r == PAIRS - 1
             if live(back):
                 transpose_g(back)
             if live(prep):
                 transpose_inputs(prep)
-            if live(r):
-                add_lora(a, 0)
-            if live(r):
-                add_lora(a, 1)
+            add_lora(a, 0)
+            add_lora(a, 1)
             if r == 1:
                 quantise_x(2)
-            if live(r):
-                copy_lora(b, 0)
-            if live(r):
-                copy_lora(b, 1)
-            if last:
-                gate(r, singly[0])
+            copy_lora(b, 0)
+            copy_lora(b, 1)
             if live(back):
-                copy_gT(back, nc.vector.tensor_copy if live(r + 1) else nc.scalar.copy)
+                copy_gT(back, nc.vector.tensor_copy)
             if live(prep):
                 copy_x(prep, nc.scalar.copy)
             if live(prep):
                 copy_xaT(prep, nc.vector.tensor_copy)
-            if live(r):
-                mx_matmul(b, 0)
-            if live(r + 1):
-                lora_matmul(a + PAIR, 0)
-            if live(r + 1):
-                lora_matmul(a + PAIR, 1)
-            if live(r):
-                mx_matmul(b, 1)
+            mx_matmul(b, 0)
+            lora_matmul(a + PAIR, 0)
+            lora_matmul(a + PAIR, 1)
+            mx_matmul(b, 1)
             if live(proj):
                 project(proj)
-            if live(r + 1):
-                copy_lora(a + PAIR, 0)
-            if live(r + 1):
-                copy_lora(a + PAIR, 1)
-            if live(r):
-                add_lora(b, 0)
-            if live(r):
-                add_lora(b, 1)
-            if live(r):
-                gate(r, singly[1] if last else both)
+            copy_lora(a + PAIR, 0)
+            copy_lora(a + PAIR, 1)
+            add_lora(b, 0)
+            add_lora(b, 1)
+            gate(r, both)
             if live(proj):
                 copy_projection(proj, nc.scalar.copy)
-            if live(r + 1):
-                lora_matmul(b + PAIR, 0)
-            if live(r + 1):
-                mx_matmul(a + PAIR, 0)
-            if live(r + 1):
-                lora_matmul(b + PAIR, 1)
-            if live(r + 1):
-                mx_matmul(a + PAIR, 1)
+            lora_matmul(b + PAIR, 0)
+            mx_matmul(a + PAIR, 0)
+            lora_matmul(b + PAIR, 1)
+            mx_matmul(a + PAIR, 1)
             if live(rnd):
-                round_g(rnd)
-            if last:
-                for tiles in singly: multiply(nc.vector, r, tiles)
+                round_g(rnd, nc.vector.tensor_copy)
             if live(prep):
                 quantise_x(prep)
             if live(back):
-                g_codes[back] = quantise(g_grouped[back], behind, "gq")
-            if live(r) and not last:
-                multiply(nc.gpsimd, r, both)
+                quantise_g(back)
+            multiply(nc.gpsimd, r, both)
+
+        def last_round(r):
+            a, b = r * PAIR, r * PAIR + 1
+            copy_v, copy_s = nc.vector.tensor_copy, nc.scalar.copy
+            transpose_g(r - 2)
+            add_lora(a, 0)
+            add_lora(a, 1)
+            copy_lora(b, 0)
+            copy_lora(b, 1)
+            gate(r, singly[0])
+            copy_gT(r - 2, copy_v)
+            mx_matmul(b, 0)
+            mx_matmul(b, 1)
+            project(r - 3)
+            add_lora(b, 0)
+            add_lora(b, 1)
+            gate(r, singly[1])
+            round_g(r - 1, copy_s)
+            copy_projection(r - 3, copy_s)
+            multiply(nc.vector, r, singly[0])
+            multiply(nc.vector, r, singly[1])
+            round_g(r, copy_v)
+            quantise_g(r - 2)
+            transpose_g(r - 1)
+            copy_gT(r - 1, copy_s)
+            transpose_g(r, tag="xT_ps")
+            project(r - 2)
+            copy_gT(r, copy_v)
+            copy_projection(r - 2, copy_s)
+            quantise_g(r - 1)
+            quantise_g(r)
+            project(r - 1, both, "mx_ps", 2)
+            copy_projection(r - 1, copy_s)
+            project(r, both, "mx_ps", 2)
+            copy_projection(r, copy_v)
 
         first_round()
-        for r in range(1, PAIRS + PROJECT_BEHIND):
+        for r in range(1, PAIRS - 1):
             one_round(r)
+        last_round(PAIRS - 1)

@@ -22,7 +22,7 @@ TILES = TOKENS // P
 PAIR = 2
 PAIRS = TILES // PAIR
 LORA_SCALING = 2.0
-LOADS = (2, 2, 4, 4, 4, 4, 4, 4, 4)
+LOADS = (4, 4, 4, 4, 4, 4, 4, 4)
 
 PREPARE_AHEAD = 2
 ROUND_BEHIND = 1
@@ -60,7 +60,7 @@ def tile_feedforward_pa_t_kernel(
         consts = ctx.enter_context(tc.tile_pool(name="consts", bufs=1))
         inputs = ctx.enter_context(tc.tile_pool(name="inputs", bufs=1))
         ahead = ctx.enter_context(tc.tile_pool(name="ahead", bufs=4))
-        work = ctx.enter_context(tc.tile_pool(name="work", bufs=3))
+        work = ctx.enter_context(tc.tile_pool(name="work", bufs=4))
         behind = ctx.enter_context(tc.tile_pool(name="behind", bufs=4))
         banks = ctx.enter_context(tc.psum_pool(name="banks", bufs=1))
         ctx.enter_context(tc.manual_schedule())
@@ -88,11 +88,11 @@ def tile_feedforward_pa_t_kernel(
         def load_inputs(n, x_queue, xa_queue):
             first, count = first_tiles[n], LOADS[n]
             tiles = slice(first, first + count)
-            x_g = inputs.tile([P, count, D], BF16, name="x_g%d" % n)
-            x_queue.dma_start(out=x_g[:], in_=x_v[:, tiles, :])
             xa_g = inputs.tile([P, 2, count, R], BF16, name="xa_g%d" % n)
             xa_queue.dma_start(out=xa_g[:, 0], in_=xa1_v[:, tiles, :])
             xa_queue.dma_start(out=xa_g[:, 1], in_=xa3_v[:, tiles, :])
+            x_g = inputs.tile([P, count, D], BF16, name="x_g%d" % n)
+            x_queue.dma_start(out=x_g[:], in_=x_v[:, tiles, :])
             for j in range(count):
                 x_in[first + j] = x_g[:, j, :]
                 xa_in[first + j] = (xa_g[:, 0, j, :], xa_g[:, 1, j, :])
@@ -123,10 +123,9 @@ def tile_feedforward_pa_t_kernel(
         load_words(w3_sb, w3_words)
         load_scales(w3_plane, w3_scales)
         load_inputs(1, nc.sync, nc.sync)
-        load_inputs(2, nc.sync, nc.sync)
         load_words(a2_sb, lora_A2_words)
         load_scales(a2_plane, lora_A2_scales)
-        for n in range(3, len(LOADS)):
+        for n in range(2, len(LOADS)):
             load_inputs(n, nc.sync, nc.sync)
 
         x_grouped = {}
@@ -156,8 +155,8 @@ def tile_feedforward_pa_t_kernel(
                 nc.tensor.transpose(bT_ps[:, c * P : (c + 1) * P], b_in[:, which, c, :], ident_bf[:])
             copy(out=bT[:, which, :], in_=bT_ps[:])
 
-        def lora_matmul(tile, which):
-            lora_ps[tile, which] = banks.tile([P, F], F32, name="lora_ps", bufs=2)
+        def lora_matmul(tile, which, tag="lora_ps", count=2):
+            lora_ps[tile, which] = banks.tile([P, F], F32, tag=tag, name="lora_ps", bufs=count)
             nc.tensor.matmul(
                 out=lora_ps[tile, which][:],
                 lhsT=xaT[tile // PAIR][:, tile % PAIR, which, :],
@@ -223,9 +222,9 @@ def tile_feedforward_pa_t_kernel(
                 for which in range(2):
                     nc.tensor.transpose(xaT_ps[:, i, which, :], xa_in[q * PAIR + i][which], ident_bf[:])
 
-        def copy_lora(tile, which):
+        def copy_lora(tile, which, copy=nc.scalar.copy):
             lora_sb[tile, which] = work.tile([P, F], F32, name="lora_sb%d" % which)
-            nc.scalar.copy(out=lora_sb[tile, which][:], in_=lora_ps[tile, which][:])
+            copy(out=lora_sb[tile, which][:], in_=lora_ps[tile, which][:])
 
         def copy_projection(q, copy, tiles=both):
             ga2_sb = behind.tile([P, PAIR, R], F32, name="ga2_sb")
@@ -326,37 +325,32 @@ def tile_feedforward_pa_t_kernel(
             transpose_xa(0)
             copy_xaT(0, nc.vector.tensor_copy)
             transpose_x(0)
-            copy_x(0, nc.scalar.copy)
-            quantise_x(0)
+            copy_x(0, nc.vector.tensor_copy)
             lora(0)
-            lora_matmul(1, 0)
-            mx_matmul(0, 0)
-            lora_matmul(1, 1)
-            mx_matmul(0, 1)
-            add_lora(0, 0)
-            add_lora(0, 1)
-            copy_lora(1, 0)
-            copy_lora(1, 1)
-            transpose_inputs(1)
-            copy_x(1, nc.scalar.copy)
-            mx_matmul(1, 0)
-            mx_matmul(1, 1)
+            transpose_xa(1)
             copy_xaT(1, nc.vector.tensor_copy)
+            quantise_x(0)
+            transpose_x(1)
+            copy_x(1, nc.vector.tensor_copy)
+            lora(1)
+            mx_matmul(0, 0)
+            mx_matmul(1, 0)
+            add_lora(0, 0)
             add_lora(1, 0)
-            add_lora(1, 1)
             quantise_x(1)
-            lora_matmul(2, 0)
-            lora_matmul(2, 1)
-            transpose_inputs(2)
-            copy_lora(2, 0)
+            lora(2)
+            mx_matmul(0, 1)
+            mx_matmul(1, 1)
             gate(0, both)
-            copy_lora(2, 1)
-            copy_x(2, nc.scalar.copy)
-            copy_xaT(2, nc.vector.tensor_copy)
+            add_lora(0, 1)
+            add_lora(1, 1)
             lora_matmul(3, 0)
+            transpose_inputs(2)
             mx_matmul(2, 0)
             lora_matmul(3, 1)
             mx_matmul(2, 1)
+            copy_x(2, nc.scalar.copy)
+            copy_xaT(2, nc.vector.tensor_copy)
             multiply(nc.gpsimd, 0, both)
 
         def one_round(r):
@@ -371,8 +365,6 @@ def tile_feedforward_pa_t_kernel(
                 transpose_inputs(prep)
             add_lora(a, 0)
             add_lora(a, 1)
-            if r == 1:
-                quantise_x(2)
             copy_lora(b, 0)
             copy_lora(b, 1)
             if live(back):
@@ -381,8 +373,10 @@ def tile_feedforward_pa_t_kernel(
                 copy_x(prep, nc.scalar.copy)
             if live(prep):
                 copy_xaT(prep, nc.vector.tensor_copy)
-            mx_matmul(b, 0)
+            if r == 1:
+                quantise_x(2)
             lora_matmul(a + PAIR, 0)
+            mx_matmul(b, 0)
             lora_matmul(a + PAIR, 1)
             mx_matmul(b, 1)
             if live(proj):

@@ -197,10 +197,10 @@ def tile_feedforward_pa_t_kernel(
 
         def transpose_g(q, tiles=both, tag="gT_ps"):
             gT_ps = banks.tile([P, PAIR, 2, P], F32, tag=tag, name="gT_ps", bufs=1)
-            g_words = g_bf[q][:].bitcast(F32).rearrange("q (u i p) -> q u i p", u=2, i=PAIR)
+            g_words = g_bf[q][:].bitcast(F32)
             for i in range(tiles.start, tiles.stop):
                 for u in range(2):
-                    nc.tensor.transpose(gT_ps[:, i, u, :], g_words[:, u, i, :], ident_f32[:])
+                    nc.tensor.transpose(gT_ps[:, i, u, :], g_words[:, i, u : F // 2 : 2], ident_f32[:])
             psum["gT"] = gT_ps
 
         def transpose_inputs(q):
@@ -282,12 +282,8 @@ def tile_feedforward_pa_t_kernel(
 
         def round_g(q, copy, tiles=both):
             if q not in g_bf:
-                g_bf[q] = behind.tile([P, PAIR * F], BF16, name="g_bf")
-            ordered = g_bf[q][:].rearrange("q (u i n e) -> q u i n e", u=2, i=PAIR, e=2)[:, :, tiles]
-            copy(
-                out=ordered.rearrange("q u i n e -> q u (i n) e"),
-                in_=g_sb[q][:, tiles, :].rearrange("q i (n u e) -> q u (i n) e", u=2, e=2),
-            )
+                g_bf[q] = behind.tile([P, PAIR, F], BF16, name="g_bf")
+            copy(out=g_bf[q][:, tiles, :], in_=g_sb[q][:, tiles, :])
 
         def quantise(source, codes, tiles):
             words, plane = codes

@@ -22,7 +22,7 @@ TILES = TOKENS // P
 PAIR = 2
 PAIRS = TILES // PAIR
 LORA_SCALING = 2.0
-LOADS = (4, 4, 4, 4, 4, 4, 4, 4)
+LOADS = (2, 2, 4, 4, 4, 4, 4, 4, 4)
 
 PREPARE_AHEAD = 2
 ROUND_BEHIND = 1
@@ -73,6 +73,8 @@ def tile_feedforward_pa_t_kernel(
         warm_in = consts.tile([P, 1], F32)
         warm_out = consts.tile([P, 1], F32)
         nc.vector.memset(warm_in[:], 0.0)
+        zeros = consts.tile([P, F], BF16)
+        nc.vector.memset(zeros[:], 0.0)
         nc.scalar.activation(out=warm_out[:], in_=warm_in[:], func=ACT.Silu)
 
         w1_plane = consts.tile([P, F], U8, align_bytes=64)
@@ -118,14 +120,15 @@ def tile_feedforward_pa_t_kernel(
         nc.sync.dma_start(out=b_in[:, 0], in_=lora_B1.rearrange("(c p) r -> p c r", p=P))
         nc.sync.dma_start(out=b_in[:, 1], in_=lora_B3.rearrange("(c p) r -> p c r", p=P))
         load_inputs(0, nc.sync, nc.sync)
+        load_inputs(1, nc.sync, nc.sync)
         load_words(w1_sb, w1_words)
         load_scales(w1_plane, w1_scales)
         load_words(w3_sb, w3_words)
         load_scales(w3_plane, w3_scales)
-        load_inputs(1, nc.sync, nc.sync)
+        load_inputs(2, nc.sync, nc.sync)
         load_words(a2_sb, lora_A2_words)
         load_scales(a2_plane, lora_A2_scales)
-        for n in range(2, len(LOADS)):
+        for n in range(3, len(LOADS)):
             load_inputs(n, nc.sync, nc.sync)
 
         x_grouped = {}
@@ -154,6 +157,11 @@ def tile_feedforward_pa_t_kernel(
             for c in range(F // P):
                 nc.tensor.transpose(bT_ps[:, c * P : (c + 1) * P], b_in[:, which, c, :], ident_bf[:])
             copy(out=bT[:, which, :], in_=bT_ps[:])
+
+        def keep_busy(count):
+            for n in range(count):
+                idle_ps = banks.tile([P, F], F32, tag="mx_ps", name="idle_ps", bufs=2)
+                nc.tensor.matmul(out=idle_ps[:], lhsT=zeros[:, 0:P], rhs=zeros[:], start=True, stop=True)
 
         def lora_matmul(tile, which, tag="lora_ps", count=2):
             lora_ps[tile, which] = banks.tile([P, F], F32, tag=tag, name="lora_ps", bufs=count)
@@ -316,10 +324,12 @@ def tile_feedforward_pa_t_kernel(
                 copy_lora(tile, which)
 
         def first_round():
+            keep_busy(4)
             transpose_lora_b(0, "gT_ps", 1, nc.vector.tensor_copy)
             transpose_lora_b(1, "ga2_ps", 1, nc.scalar.copy)
             transpose_xa(0)
             copy_xaT(0, nc.vector.tensor_copy)
+            keep_busy(1)
             transpose_x(0)
             copy_x(0, nc.vector.tensor_copy)
             lora(0)
@@ -394,7 +404,8 @@ def tile_feedforward_pa_t_kernel(
                 quantise_x(prep)
             if live(back):
                 quantise_g(back)
-            multiply(nc.gpsimd, r, both)
+            if True:
+                multiply(nc.gpsimd, r, both)
 
         def last_round(r):
             a, b = r * PAIR, r * PAIR + 1

@@ -208,7 +208,7 @@ def tile_feedforward_pa_t_kernel(
             g_words = g_bf[q][:].bitcast(F32)
             for i in range(tiles.start, tiles.stop):
                 for u in range(2):
-                    nc.tensor.transpose(gT_ps[:, i, u, :], g_words[:, i, u : F // 2 : 2], ident_f32[:])
+                    nc.tensor.transpose(gT_ps[:, i, u, :], g_words[:, u, i, :], ident_f32[:])
             psum["gT"] = gT_ps
 
         def transpose_inputs(q):
@@ -290,8 +290,11 @@ def tile_feedforward_pa_t_kernel(
 
         def round_g(q, copy, tiles=both):
             if q not in g_bf:
-                g_bf[q] = behind.tile([P, PAIR, F], BF16, name="g_bf")
-            copy(out=g_bf[q][:, tiles, :], in_=g_sb[q][:, tiles, :])
+                g_bf[q] = behind.tile([P, 2, PAIR, F // 2], BF16, name="g_bf")
+            copy(
+                out=g_bf[q][:, :, tiles].rearrange("q u i (n e) -> q (i n) u e", e=2),
+                in_=g_sb[q][:, tiles, :].rearrange("q i (n u e) -> q (i n) u e", u=2, e=2),
+            )
 
         def quantise(source, codes, tiles):
             words, plane = codes

@@ -376,6 +376,8 @@ def tile_feedforward_pa_t_kernel(
             add_lora(a, 1)
             copy_lora(b, 0)
             copy_lora(b, 1)
+            if live(proj - 1):
+                copy_projection(proj - 1, nc.scalar.copy)
             if live(back):
                 copy_gT(back, nc.vector.tensor_copy)
             if live(prep):
@@ -395,8 +397,6 @@ def tile_feedforward_pa_t_kernel(
             add_lora(b, 0)
             add_lora(b, 1)
             gate(r, both)
-            if live(proj):
-                copy_projection(proj, nc.scalar.copy)
             lora_matmul(b + PAIR, 0)
             mx_matmul(a + PAIR, 0)
             lora_matmul(b + PAIR, 1)
@@ -418,25 +418,29 @@ def tile_feedforward_pa_t_kernel(
             add_lora(a, 1)
             copy_lora(b, 0)
             copy_lora(b, 1)
+            copy_projection(r - 4, copy_s)
             gate(r, singly[0])
-            copy_gT(r - 2, copy_v)
+            copy_gT(r - 2, copy_s)
             mx_matmul(b, 0)
             mx_matmul(b, 1)
             project(r - 3)
             add_lora(b, 0)
             add_lora(b, 1)
             gate(r, singly[1])
-            round_g(r - 1, copy_s)
+            round_g(r - 1, copy_s, singly[0])
             copy_projection(r - 3, copy_s)
             multiply(nc.vector, r, singly[0])
             multiply(nc.vector, r, singly[1])
+            round_g(r - 1, copy_v, singly[1])
             round_g(r, copy_v)
             quantise_g(r - 2)
             transpose_g(r - 1)
             copy_gT(r - 1, copy_s)
-            transpose_g(r, tag="xT_ps")
+            transpose_g(r, singly[0], "xT_ps")
+            copy_gT(r, copy_v, singly[0])
+            transpose_g(r, singly[1], "xaT_ps")
+            copy_gT(r, copy_v, singly[1])
             project(r - 2)
-            copy_gT(r, copy_v)
             copy_projection(r - 2, copy_s)
             quantise_g(r - 1)
             quantise_g(r)

@@ -131,8 +131,8 @@ def tile_feedforward_pa_t_kernel(
         for n in range(3, len(LOADS)):
             load_inputs(n, nc.sync, nc.sync)
 
-        x_grouped = {}
-        x_codes = {}
+        grouped_of = {}
+        codes_of = {}
         xaT = {}
         lora_ps = {}
         lora_sb = {}
@@ -141,8 +141,6 @@ def tile_feedforward_pa_t_kernel(
         s1 = {}
         g_sb = {}
         g_bf = {}
-        g_grouped = {}
-        g_codes = {}
         psum = {}
         bT = consts.tile([P, 2, F], BF16)
         weights = ((w1_sb, w1_plane), (w3_sb, w3_plane))
@@ -174,7 +172,7 @@ def tile_feedforward_pa_t_kernel(
             )
 
         def mx_matmul(tile, which):
-            words, plane = x_codes[tile // PAIR]
+            words, plane = codes_of["x", tile // PAIR]
             cols = slice(tile % PAIR * P, (tile % PAIR + 1) * P)
             w_sb, w_plane = weights[which]
             mx_ps[tile, which] = banks.tile([P, F], F32, name="mx_ps", bufs=2)
@@ -189,7 +187,7 @@ def tile_feedforward_pa_t_kernel(
             )
 
         def project(q, tiles=both, tag="ga2_ps", count=1):
-            words, plane = g_codes[q]
+            words, plane = codes_of["g", q]
             psum["ga2"] = banks.tile([P, PAIR, R], F32, tag=tag, name="ga2_ps", bufs=count)
             for i in range(tiles.start, tiles.stop):
                 cols = slice(i * P, (i + 1) * P)
@@ -242,12 +240,10 @@ def tile_feedforward_pa_t_kernel(
             )
 
         def copy_x(q, copy):
-            grouped = ahead.tile([P, PAIR * P * PACK], BF16, align_bytes=64, name="x_grouped")
             copy(
-                out=grouped[:].bitcast(F32).rearrange("p (i r u) -> p i r u", i=PAIR, u=2),
+                out=grouped_of["x", q].bitcast(F32).rearrange("p (i r u) -> p i r u", i=PAIR, u=2),
                 in_=psum["xT"][:].rearrange("p i u r -> p i r u"),
             )
-            x_grouped[q] = grouped
 
         def gate(q, tiles):
             if q not in s1:
@@ -276,9 +272,7 @@ def tile_feedforward_pa_t_kernel(
             )
 
         def copy_gT(q, copy, tiles=both):
-            if q not in g_grouped:
-                g_grouped[q] = behind.tile([P, PAIR * P * PACK], BF16, align_bytes=64, name="g_grouped")
-            grouped_words = g_grouped[q][:].bitcast(F32).rearrange("p (i r u) -> p i r u", i=PAIR, u=2)
+            grouped_words = grouped_of["g", q].bitcast(F32).rearrange("p (i r u) -> p i r u", i=PAIR, u=2)
             copy(
                 out=grouped_words[:, tiles],
                 in_=psum["gT"][:].rearrange("p i u r -> p i r u")[:, tiles],
@@ -296,29 +290,24 @@ def tile_feedforward_pa_t_kernel(
                 in_=g_sb[q][:, tiles, :].rearrange("q i (n u e) -> q (i n) u e", u=2, e=2),
             )
 
-        def quantise(source, codes, tiles):
-            words, plane = codes
-            cols = slice(tiles.start * P, tiles.stop * P)
-            nc.vector.quantize_mx(
-                out=words[:, cols].bitcast(FP8X4),
-                scales=plane[:, cols],
-                in_=source[:, tiles.start * P * PACK : tiles.stop * P * PACK],
-            )
+        def place(*members):
+            width = PAIR * P
+            count = len(members)
+            grouped = ahead.tile([P, count * width * PACK], BF16, align_bytes=64, name="grouped")
+            words = ahead.tile([P, count * width], U32, align_bytes=64, name="words")
+            plane = ahead.tile([P, count * width], U8, align_bytes=64, name="plane")
+            for j in range(count):
+                cols = slice(j * width, (j + 1) * width)
+                grouped_of[members[j]] = grouped[:, j * width * PACK : (j + 1) * width * PACK]
+                codes_of[members[j]] = (words[:, cols], plane[:, cols])
+            return grouped[:], words[:], plane[:]
 
-        def quantise_x(q):
-            x_codes[q] = (
-                ahead.tile([P, PAIR * P], U32, align_bytes=64, name="xq_words"),
-                ahead.tile([P, PAIR * P], U8, align_bytes=64, name="xq_plane"),
-            )
-            quantise(x_grouped[q], x_codes[q], both)
+        def quantise(grouped, words, plane):
+            nc.vector.quantize_mx(out=words.bitcast(FP8X4), scales=plane, in_=grouped)
 
-        def quantise_g(q, tiles=both):
-            if q not in g_codes:
-                g_codes[q] = (
-                    behind.tile([P, PAIR * P], U32, align_bytes=64, name="gq_words"),
-                    behind.tile([P, PAIR * P], U8, align_bytes=64, name="gq_plane"),
-                )
-            quantise(g_grouped[q], g_codes[q], tiles)
+        def quantise_g(q):
+            words, plane = codes_of["g", q]
+            quantise(grouped_of["g", q], words, plane)
 
 
         def lora(tile):
@@ -334,19 +323,21 @@ def tile_feedforward_pa_t_kernel(
             copy_xaT(0, nc.vector.tensor_copy)
             keep_busy(1)
             transpose_x(0)
+            pair_0 = place(("x", 0))
             copy_x(0, nc.vector.tensor_copy)
             lora(0)
             transpose_xa(1)
             copy_xaT(1, nc.vector.tensor_copy)
-            quantise_x(0)
+            quantise(*pair_0)
             transpose_x(1)
+            pair_1 = place(("x", 1))
             copy_x(1, nc.vector.tensor_copy)
             lora(1)
             mx_matmul(0, 0)
             mx_matmul(1, 0)
             add_lora(0, 0)
             add_lora(1, 0)
-            quantise_x(1)
+            quantise(*pair_1)
             lora(2)
             mx_matmul(0, 1)
             mx_matmul(1, 1)
@@ -358,6 +349,7 @@ def tile_feedforward_pa_t_kernel(
             mx_matmul(2, 0)
             lora_matmul(3, 1)
             mx_matmul(2, 1)
+            place(("x", 2))
             copy_x(2, nc.scalar.copy)
             copy_xaT(2, nc.vector.tensor_copy)
             multiply(nc.gpsimd, 0, both)
@@ -378,6 +370,8 @@ def tile_feedforward_pa_t_kernel(
             copy_lora(b, 1)
             if live(proj - 1):
                 copy_projection(proj - 1, nc.scalar.copy)
+            if True:
+                shared = place(*[m for m in (("x", prep), ("g", back)) if live(m[1])])
             if live(back):
                 copy_gT(back, nc.vector.tensor_copy)
             if live(prep):
@@ -385,7 +379,7 @@ def tile_feedforward_pa_t_kernel(
             if live(prep):
                 copy_xaT(prep, nc.vector.tensor_copy)
             if r == 1:
-                quantise_x(2)
+                quantise(grouped_of["x", 2], *codes_of["x", 2])
             lora_matmul(a + PAIR, 0)
             mx_matmul(b, 0)
             lora_matmul(a + PAIR, 1)
@@ -403,16 +397,16 @@ def tile_feedforward_pa_t_kernel(
             mx_matmul(a + PAIR, 1)
             if live(rnd):
                 round_g(rnd, nc.vector.tensor_copy)
-            if live(prep):
-                quantise_x(prep)
-            if live(back):
-                quantise_g(back)
+            if True:
+                quantise(*shared)
             if True:
                 multiply(nc.gpsimd, r, both)
 
         def last_round(r):
             a, b = r * PAIR, r * PAIR + 1
             copy_v, copy_s = nc.vector.tensor_copy, nc.scalar.copy
+            for q in (r - 2, r - 1, r):
+                place(("g", q))
             transpose_g(r - 2)
             add_lora(a, 0)
             add_lora(a, 1)

from contextlib import ExitStack

import concourse.mybir as mybir
from concourse.masks import make_identity

F32 = mybir.dt.float32
BF16 = mybir.dt.bfloat16
I32 = mybir.dt.int32
U32 = mybir.dt.uint32
U8 = mybir.dt.uint8
FP8X4 = mybir.dt.float8_e4m3fn_x4
ACT = mybir.ActivationFunctionType
ALU = mybir.AluOpType

P = 128
PACK = 4
TOKENS = 4 * 1024
D = 512
F = 512
R = 128
TILES = TOKENS // P
PAIR = 2
PAIRS = TILES // PAIR
LORA_SCALING = 2.0
LOADS = (2, 2, 4, 4, 4, 4, 4, 4, 4)

PREPARE_AHEAD = 2
ROUND_BEHIND = 1
TRANSPOSE_BEHIND = 2
PROJECT_BEHIND = 3

FLOPS = 2 * TOKENS * (2 * D * F + 2 * R * F + F * R)


def tile_feedforward_pa_t_kernel(
    tc,
    x,
    w1_words,
    w1_scales,
    w3_words,
    w3_scales,
    xa1,
    xa3,
    lora_B1,
    lora_B3,
    lora_A2_words,
    lora_A2_scales,
    out_0,
    out_1,
):
    nc = tc.nc

    x_v = x.flatten_outer_dims().rearrange("(p i) d -> p i d", i=TILES)
    xa1_v = xa1.flatten_outer_dims().rearrange("(p i) r -> p i r", i=TILES)
    xa3_v = xa3.flatten_outer_dims().rearrange("(p i) r -> p i r", i=TILES)
    g_v = out_0.flatten_outer_dims().rearrange("(p i) f -> p i f", i=TILES)
    ga2_v = out_1.flatten_outer_dims().rearrange("(p i) r -> p i r", i=TILES)

    with ExitStack() as ctx:
        consts = ctx.enter_context(tc.tile_pool(name="consts", bufs=1))
        inputs = ctx.enter_context(tc.tile_pool(name="inputs", bufs=1))
        ahead = ctx.enter_context(tc.tile_pool(name="ahead", bufs=4))
        work = ctx.enter_context(tc.tile_pool(name="work", bufs=4))
        behind = ctx.enter_context(tc.tile_pool(name="behind", bufs=4))
        banks = ctx.enter_context(tc.psum_pool(name="banks", bufs=1))
        ctx.enter_context(tc.manual_schedule())

        ident_bf = consts.tile([P, P], BF16)
        make_identity(nc, ident_bf[:])
        ident_f32 = consts.tile([P, P], F32)
        make_identity(nc, ident_f32[:])

        warm_in = consts.tile([P, 1], F32)
        warm_out = consts.tile([P, 1], F32)
        nc.vector.memset(warm_in[:], 0.0)
        zeros = consts.tile([P, F], BF16)
        nc.vector.memset(zeros[:], 0.0)
        nc.scalar.activation(out=warm_out[:], in_=warm_in[:], func=ACT.Silu)

        w1_plane = consts.tile([P, F], U8, align_bytes=64)
        w3_plane = consts.tile([P, F], U8, align_bytes=64)
        a2_plane = consts.tile([P, R], U8, align_bytes=64)
        for plane in (w1_plane, w3_plane, a2_plane):
            nc.vector.memset(plane[:].bitcast(I32), 0)

        x_in = {}
        xa_in = {}
        first_tiles = [sum(LOADS[:n]) for n in range(len(LOADS))]

        def load_inputs(n, x_queue, xa_queue):
            first, count = first_tiles[n], LOADS[n]
            tiles = slice(first, first + count)
            xa_g = inputs.tile([P, 2, count, R], BF16, name="xa_g%d" % n)
            xa_queue.dma_start(out=xa_g[:, 0], in_=xa1_v[:, tiles, :])
            xa_queue.dma_start(out=xa_g[:, 1], in_=xa3_v[:, tiles, :])
            x_g = inputs.tile([P, count, D], BF16, name="x_g%d" % n)
            x_queue.dma_start(out=x_g[:], in_=x_v[:, tiles, :])
            for j in range(count):
                x_in[first + j] = x_g[:, j, :]
                xa_in[first + j] = (xa_g[:, 0, j, :], xa_g[:, 1, j, :])

        def load_scales(plane, scales):
            for quad in range(4):
                nc.sync.dma_start(
                    out=plane[32 * quad : 32 * quad + 4, :].bitcast(I32),
                    in_=scales[0, 4 * quad : 4 * quad + 4, :].bitcast(I32),
                )

        def load_words(words_sb, words):
            nc.sync.dma_start(
                out=words_sb[:].bitcast(I32),
                in_=words[0].rearrange("p n t -> p (n t)").bitcast(I32),
            )

        w1_sb = consts.tile([P, F * PACK], U8, align_bytes=64)
        w3_sb = consts.tile([P, F * PACK], U8, align_bytes=64)
        a2_sb = consts.tile([P, R * PACK], U8, align_bytes=64)
        b_in = consts.tile([P, 2, F // P, R], BF16)

        nc.sync.dma_start(out=b_in[:, 0], in_=lora_B1.rearrange("(c p) r -> p c r", p=P))
        nc.sync.dma_start(out=b_in[:, 1], in_=lora_B3.rearrange("(c p) r -> p c r", p=P))
        load_inputs(0, nc.sync, nc.sync)
        load_inputs(1, nc.sync, nc.sync)
        load_words(w1_sb, w1_words)
        load_scales(w1_plane, w1_scales)
        load_words(w3_sb, w3_words)
        load_scales(w3_plane, w3_scales)
        load_inputs(2, nc.sync, nc.sync)
        load_words(a2_sb, lora_A2_words)
        load_scales(a2_plane, lora_A2_scales)
        for n in range(3, len(LOADS)):
            load_inputs(n, nc.sync, nc.sync)

        grouped_of = {}
        codes_of = {}
        xaT = {}
        lora_ps = {}
        lora_sb = {}
        mx_ps = {}
        h_sb = {}
        s1 = {}
        g_sb = {}
        g_bf = {}
        psum = {}
        bT = consts.tile([P, 2, F], BF16)
        weights = ((w1_sb, w1_plane), (w3_sb, w3_plane))
        both = slice(0, PAIR)
        singly = [slice(i, i + 1) for i in range(PAIR)]

        def live(q):
            return 0 <= q < PAIRS

        def transpose_lora_b(which, tag, nbanks, copy):
            bT_ps = banks.tile([P, F], BF16, tag=tag, name="bT_ps", bufs=nbanks)
            for c in range(F // P):
                nc.tensor.transpose(bT_ps[:, c * P : (c + 1) * P], b_in[:, which, c, :], ident_bf[:])
            copy(out=bT[:, which, :], in_=bT_ps[:])

        def keep_busy(count):
            for n in range(count):
                idle_ps = banks.tile([P, F], F32, tag="mx_ps", name="idle_ps", bufs=2)
                nc.tensor.matmul(out=idle_ps[:], lhsT=zeros[:, 0:P], rhs=zeros[:], start=True, stop=True)

        def lora_matmul(tile, which, tag="lora_ps", count=2):
            lora_ps[tile, which] = banks.tile([P, F], F32, tag=tag, name="lora_ps", bufs=count)
            nc.tensor.matmul(
                out=lora_ps[tile, which][:],
                lhsT=xaT[tile // PAIR][:, tile % PAIR, which, :],
                rhs=bT[:, which, :],
                start=True,
                stop=True,
            )

        def mx_matmul(tile, which):
            words, plane = codes_of["x", tile // PAIR]
            cols = slice(tile % PAIR * P, (tile % PAIR + 1) * P)
            w_sb, w_plane = weights[which]
            mx_ps[tile, which] = banks.tile([P, F], F32, name="mx_ps", bufs=2)
            nc.tensor.matmul_mx(
                out=mx_ps[tile, which][:],
                lhsT=words[:, cols].bitcast(FP8X4),
                lhsT_scale=plane[:, cols],
                rhs=w_sb[:].bitcast(FP8X4),
                rhs_scale=w_plane[:],
                start=True,
                stop=True,
            )

        def project(q, tiles=both, tag="ga2_ps", count=1):
            words, plane = codes_of["g", q]
            psum["ga2"] = banks.tile([P, PAIR, R], F32, tag=tag, name="ga2_ps", bufs=count)
            for i in range(tiles.start, tiles.stop):
                cols = slice(i * P, (i + 1) * P)
                nc.tensor.matmul_mx(
                    out=psum["ga2"][:, i, :],
                    lhsT=words[:, cols].bitcast(FP8X4),
                    lhsT_scale=plane[:, cols],
                    rhs=a2_sb[:].bitcast(FP8X4),
                    rhs_scale=a2_plane[:],
                    start=True,
                    stop=True,
                )

        def transpose_g(q, tiles=both, tag="gT_ps"):
            gT_ps = banks.tile([P, PAIR, 2, P], F32, tag=tag, name="gT_ps", bufs=1)
            g_words = g_bf[q][:].bitcast(F32)
            for i in range(tiles.start, tiles.stop):
                for u in range(2):
                    nc.tensor.transpose(gT_ps[:, i, u, :], g_words[:, u, i, :], ident_f32[:])
            psum["gT"] = gT_ps

        def transpose_inputs(q):
            transpose_x(q)
            transpose_xa(q)

        def transpose_x(q):
            xT_ps = banks.tile([P, PAIR, 2, P], F32, tag="xT_ps", name="xT_ps", bufs=1)
            psum["xT"] = xT_ps
            for i in range(PAIR):
                x_words = x_in[q * PAIR + i].bitcast(F32)
                for u in range(2):
                    nc.tensor.transpose(xT_ps[:, i, u, :], x_words[:, u : D // 2 : 2], ident_f32[:])

        def transpose_xa(q):
            xaT_ps = banks.tile([P, PAIR, 2, P], BF16, tag="xaT_ps", name="xaT_ps", bufs=1)
            psum["xaT"] = xaT_ps
            for i in range(PAIR):
                for which in range(2):
                    nc.tensor.transpose(xaT_ps[:, i, which, :], xa_in[q * PAIR + i][which], ident_bf[:])

        def copy_lora(tile, which, copy=nc.scalar.copy):
            lora_sb[tile, which] = work.tile([P, F], F32, name="lora_sb%d" % which)
            copy(out=lora_sb[tile, which][:], in_=lora_ps[tile, which][:])

        def copy_projection(q, copy, tiles=both):
            ga2_sb = behind.tile([P, PAIR, R], F32, name="ga2_sb")
            copy(out=ga2_sb[:, tiles, :], in_=psum["ga2"][:, tiles, :])
            nc.sync.dma_start(
                out=ga2_v[:, q * PAIR + tiles.start : q * PAIR + tiles.stop, :], in_=ga2_sb[:, tiles, :]
            )

        def copy_x(q, copy):
            copy(
                out=grouped_of["x", q].bitcast(F32).rearrange("p (i r u) -> p i r u", i=PAIR, u=2),
                in_=psum["xT"][:].rearrange("p i u r -> p i r u"),
            )

        def gate(q, tiles):
            if q not in s1:
                s1[q] = work.tile([P, PAIR, F], F32, name="s1")
            nc.scalar.activation(out=s1[q][:, tiles, :], in_=h_sb[q][0][:, tiles, :], func=ACT.Silu)

        def multiply(engine, q, tiles):
            if q not in g_sb:
                g_sb[q] = behind.tile([P, PAIR, F], F32, name="g_sb")
            engine.tensor_tensor(out=g_sb[q][:, tiles, :], in0=s1[q][:, tiles, :], in1=h_sb[q][1][:, tiles, :], op=ALU.mult)
            nc.sync.dma_start(
                out=g_v[:, q * PAIR + tiles.start : q * PAIR + tiles.stop, :], in_=g_sb[q][:, tiles, :]
            )

        def add_lora(tile, which):
            q, i = tile // PAIR, tile % PAIR
            if q not in h_sb:
                h_sb[q] = [work.tile([P, PAIR, F], F32, name="h%d" % w) for w in range(2)]
            nc.vector.scalar_tensor_tensor(
                out=h_sb[q][which][:, i, :],
                in0=lora_sb[tile, which][:],
                scalar=LORA_SCALING,
                in1=mx_ps[tile, which][:],
                op0=ALU.mult,
                op1=ALU.add,
            )

        def copy_gT(q, copy, tiles=both):
            grouped_words = grouped_of["g", q].bitcast(F32).rearrange("p (i r u) -> p i r u", i=PAIR, u=2)
            copy(
                out=grouped_words[:, tiles],
                in_=psum["gT"][:].rearrange("p i u r -> p i r u")[:, tiles],
            )

        def copy_xaT(q, copy):
            xaT[q] = ahead.tile([P, PAIR, 2, P], BF16, name="xaT_sb")
            copy(out=xaT[q][:], in_=psum["xaT"][:])

        def round_g(q, copy, tiles=both):
            if q not in g_bf:
                g_bf[q] = behind.tile([P, 2, PAIR, F // 2], BF16, name="g_bf")
            copy(
                out=g_bf[q][:, :, tiles].rearrange("q u i (n e) -> q (i n) u e", e=2),
                in_=g_sb[q][:, tiles, :].rearrange("q i (n u e) -> q (i n) u e", u=2, e=2),
            )

        def place(*members):
            width = PAIR * P
            count = len(members)
            grouped = ahead.tile([P, count * width * PACK], BF16, align_bytes=64, name="grouped")
            words = ahead.tile([P, count * width], U32, align_bytes=64, name="words")
            plane = ahead.tile([P, count * width], U8, align_bytes=64, name="plane")
            for j in range(count):
                cols = slice(j * width, (j + 1) * width)
                grouped_of[members[j]] = grouped[:, j * width * PACK : (j + 1) * width * PACK]
                codes_of[members[j]] = (words[:, cols], plane[:, cols])
            return grouped[:], words[:], plane[:]

        def quantise(grouped, words, plane):
            nc.vector.quantize_mx(out=words.bitcast(FP8X4), scales=plane, in_=grouped)

        def quantise_g(q):
            words, plane = codes_of["g", q]
            quantise(grouped_of["g", q], words, plane)


        def lora(tile):
            for which in range(2):
                lora_matmul(tile, which)
                copy_lora(tile, which)

        def first_round():
            keep_busy(4)
            transpose_lora_b(0, "gT_ps", 1, nc.vector.tensor_copy)
            transpose_lora_b(1, "ga2_ps", 1, nc.scalar.copy)
            transpose_xa(0)
            copy_xaT(0, nc.vector.tensor_copy)
            keep_busy(1)
            transpose_x(0)
            pair_0 = place(("x", 0))
            copy_x(0, nc.vector.tensor_copy)
            lora(0)
            transpose_xa(1)
            copy_xaT(1, nc.vector.tensor_copy)
            quantise(*pair_0)
            transpose_x(1)
            pair_1 = place(("x", 1))
            copy_x(1, nc.vector.tensor_copy)
            lora(1)
            mx_matmul(0, 0)
            mx_matmul(1, 0)
            add_lora(0, 0)
            add_lora(1, 0)
            quantise(*pair_1)
            lora(2)
            mx_matmul(0, 1)
            mx_matmul(1, 1)
            gate(0, both)
            add_lora(0, 1)
            add_lora(1, 1)
            lora_matmul(3, 0)
            transpose_inputs(2)
            mx_matmul(2, 0)
            lora_matmul(3, 1)
            mx_matmul(2, 1)
            place(("x", 2))
            copy_x(2, nc.scalar.copy)
            copy_xaT(2, nc.vector.tensor_copy)
            multiply(nc.gpsimd, 0, both)

        def one_round(r):
            prep = r + PREPARE_AHEAD
            rnd = r - ROUND_BEHIND
            back = r - TRANSPOSE_BEHIND
            proj = r - PROJECT_BEHIND
            a, b = r * PAIR, r * PAIR + 1
            if live(back):
                transpose_g(back)
            if live(prep):
                transpose_inputs(prep)
            add_lora(a, 0)
            add_lora(a, 1)
            copy_lora(b, 0)
            copy_lora(b, 1)
            if live(proj - 1):
                copy_projection(proj - 1, nc.scalar.copy)
            if True:
                shared = place(*[m for m in (("x", prep), ("g", back)) if live(m[1])])
            if live(back):
                copy_gT(back, nc.vector.tensor_copy)
            if live(prep):
                copy_x(prep, nc.scalar.copy)
            if live(prep):
                copy_xaT(prep, nc.vector.tensor_copy)
            if r == 1:
                quantise(grouped_of["x", 2], *codes_of["x", 2])
            lora_matmul(a + PAIR, 0)
            mx_matmul(b, 0)
            lora_matmul(a + PAIR, 1)
            mx_matmul(b, 1)
            if live(proj):
                project(proj)
            copy_lora(a + PAIR, 0)
            copy_lora(a + PAIR, 1)
            add_lora(b, 0)
            add_lora(b, 1)
            gate(r, both)
            lora_matmul(b + PAIR, 0)
            mx_matmul(a + PAIR, 0)
            lora_matmul(b + PAIR, 1)
            mx_matmul(a + PAIR, 1)
            if live(rnd):
                round_g(rnd, nc.vector.tensor_copy)
            if True:
                quantise(*shared)
            if True:
                multiply(nc.gpsimd, r, both)

        def last_round(r):
            a, b = r * PAIR, r * PAIR + 1
            copy_v, copy_s = nc.vector.tensor_copy, nc.scalar.copy
            for q in (r - 2, r - 1, r):
                place(("g", q))
            transpose_g(r - 2)
            add_lora(a, 0)
            add_lora(a, 1)
            copy_lora(b, 0)
            copy_lora(b, 1)
            copy_projection(r - 4, copy_s)
            gate(r, singly[0])
            copy_gT(r - 2, copy_s)
            mx_matmul(b, 0)
            mx_matmul(b, 1)
            project(r - 3)
            add_lora(b, 0)
            add_lora(b, 1)
            gate(r, singly[1])
            round_g(r - 1, copy_s, singly[0])
            copy_projection(r - 3, copy_s)
            multiply(nc.vector, r, singly[0])
            multiply(nc.vector, r, singly[1])
            round_g(r - 1, copy_v, singly[1])
            round_g(r, copy_v)
            quantise_g(r - 2)
            transpose_g(r - 1)
            copy_gT(r - 1, copy_s)
            transpose_g(r, singly[0], "xT_ps")
            copy_gT(r, copy_v, singly[0])
            transpose_g(r, singly[1], "xaT_ps")
            copy_gT(r, copy_v, singly[1])
            project(r - 2)
            copy_projection(r - 2, copy_s)
            quantise_g(r - 1)
            quantise_g(r)
            project(r - 1, both, "mx_ps", 2)
            copy_projection(r - 1, copy_s)
            project(r, both, "mx_ps", 2)
            copy_projection(r, copy_v)

        first_round()
        for r in range(1, PAIRS - 1):
            one_round(r)
        last_round(PAIRS - 1)
